import numpy as np
import ml_dtypes


def mxq(x, axis, fmt="e4m3"):
    dtype, down = {"e4m3": (ml_dtypes.float8_e4m3fn, 7), "e5m2": (ml_dtypes.float8_e5m2, 14)}[fmt]
    v = np.moveaxis(np.asarray(x, np.float32).astype(ml_dtypes.bfloat16).astype(np.float64), axis, -1)
    blocks = v.reshape(v.shape[:-1] + (-1, 32))
    amax = np.abs(blocks).max(-1, keepdims=True)
    byte = np.maximum(np.where(amax > 0, np.frexp(amax)[1] - 1 + 127, 0) - down, 1)
    scale = np.exp2(byte - 127.0)
    codes = (blocks / scale).astype(np.float32).astype(dtype).astype(np.float64)
    return np.moveaxis((codes * scale).reshape(v.shape), -1, axis)


WIDE = False


def mx_kscale(k):
    if not WIDE:
        return np.ones(k)
    levels = np.array([10, -10, 5, -5, 0])
    if k % 512:
        return np.exp2(np.random.permutation(np.resize(levels, k // 32))).repeat(32)
    a = np.empty((k // 512, 16))
    for p in range(k // 512):
        a[p, :8] = np.random.permutation(np.resize(levels, 8))
        for g in range(8):
            far = levels[np.abs(levels - a[p, g]) >= 10]
            a[p, g + 8] = far[np.random.randint(len(far))]
    return np.exp2(a.ravel()).repeat(32)


BF16 = ml_dtypes.bfloat16


def bf(x):
    return np.asarray(x, np.float32).astype(BF16)


def f64(x):
    return np.asarray(x).astype(np.float64)


B, F, H, W, D, NH, PF, PH, PW, CF, TF, LR = 1, 40, 8, 8, 512, 4, 8, 4, 4, 6, 5, 18
S = F * H * W
HD = D // NH
EPS = 1e-5


def rms_norm(y, g):
    v = np.mean(np.square(y), axis=-1, keepdims=True)
    return y / np.sqrt(v + EPS) * g


def rope(y, freqs):
    yr = y.reshape(B, S, NH, HD // 2, 2)
    c, s = freqs[..., 0], freqs[..., 1]
    a, d = yr[..., 0], yr[..., 1]
    return np.stack([a * c - d * s, a * s + d * c], axis=-1).reshape(B, S, D)


def window_order(y):
    y = y.reshape(B, F // PF, PF, H // PH, PH, W // PW, PW, D)
    return y.transpose(0, 1, 3, 5, 2, 4, 6, 7).reshape(B, S, D)


def draw0():
    s = mx_kscale(D)
    ang = np.random.uniform(0.0, 2.0 * np.pi, (S, 1, HD // 2))
    return {"x": bf(np.random.standard_normal((B, S, D)) * s),
            "freqs": bf(np.stack([np.cos(ang), np.sin(ang)], axis=-1)),
            "w": bf(np.random.standard_normal((D, D)) / np.sqrt(D) / s[:, None]),
            "b": bf(0.1 * np.random.standard_normal(D)),
            "g": bf(1.0 + 0.1 * np.random.standard_normal(D))}


def core(x, freqs, w, b, g):
    y = (mxq(f64(x), 2, "e4m3") @ mxq(f64(w), 0, "e4m3")) + f64(b)
    return window_order(rope(rms_norm(y, f64(g)), f64(freqs)))


def e4m3fn_bytes(y):
    return np.clip(np.asarray(y, np.float64), -448.0, 448.0).astype(np.float32).astype(ml_dtypes.float8_e4m3fn).view(np.uint8)


def e4m3fn_values(b):
    return np.asarray(b, np.uint8).view(ml_dtypes.float8_e4m3fn).astype(np.float64)


def setup_inputs():
    d = draw0()
    x0 = np.asarray(d['x']).astype(np.float64)
    s = (np.max(np.abs(x0), axis=(0, 1), keepdims=True) / 448.0).astype(np.float32)
    out = {}
    for k, v in d.items():
        if k == 'x':
            out['x_bytes'] = e4m3fn_bytes(x0 / s.astype(np.float64))
            out['x_scale'] = s
        else:
            out[k] = v
    return out


def reference(x_bytes, x_scale, freqs, w, b, g):
    return core(e4m3fn_values(x_bytes) * x_scale.astype(np.float64), freqs, w, b, g)

@@ -1,0 +1,269 @@
+from contextlib import ExitStack
+
+import concourse.mybir as mybir
+
+F32 = mybir.dt.float32
+BF16 = mybir.dt.bfloat16
+I32 = mybir.dt.int32
+U32 = mybir.dt.uint32
+U8 = mybir.dt.uint8
+FP8 = mybir.dt.float8_e4m3fn
+FP8X4 = mybir.dt.float8_e4m3fn_x4
+ALU = mybir.AluOpType
+ACT = mybir.ActivationFunctionType
+AX = mybir.AxisListType
+
+P = 128
+TOKENS = 2560
+D = 512
+HEADS = 4
+PAIRS = 64
+PACK = 4
+GROUPS = 5
+TILES = 4
+EPS = 1e-5
+FLOPS = 2 * TOKENS * D * D
+
+A_LEAD = 3
+C_LAG = 2
+MX_REPEATS = 2
+
+
+def tile_selfattention_pa_kernel(tc, x_bytes, x_scale, freqs, w, b, g, out):
+    nc = tc.nc
+    x_first = x_bytes.rearrange("o (g p q) k -> (o g) p (q k)", p=P, q=TILES)
+    x_by_partition = x_bytes.rearrange("o (g p q) k -> p (o g) (q k)", p=P, q=TILES)
+    freqs_by_window = freqs.rearrange(
+        "(g fi ho hi wo q) o j f -> g ho wo fi hi (q o j f)", g=GROUPS, fi=8, ho=2, hi=4, wo=2, q=TILES
+    )
+    out_by_tile = out.rearrange("o (g hw a q) f -> (o g) q a hw f", g=GROUPS, hw=4, a=32, q=TILES)
+
+    with ExitStack() as ctx:
+        const = ctx.enter_context(tc.tile_pool(name="const", bufs=1))
+        per_group = ctx.enter_context(tc.tile_pool(name="per_group", bufs=GROUPS))
+        per_head = ctx.enter_context(tc.tile_pool(name="per_head", bufs=4 * HEADS))
+        per_tile = ctx.enter_context(tc.tile_pool(name="per_tile", bufs=6))
+        psum_a = ctx.enter_context(tc.psum_pool(name="psum_a", bufs=2))
+        psum_acc = ctx.enter_context(tc.psum_pool(name="psum_acc", bufs=2))
+        psum_sq = ctx.enter_context(tc.psum_pool(name="psum_sq", bufs=2))
+        psum_c = ctx.enter_context(tc.psum_pool(name="psum_c", bufs=2))
+
+        x_bytes_0 = const.tile([P, TILES * D], U8, name="x_bytes_0")
+        x_bytes_rest = const.tile([P, GROUPS - 1, TILES * D], U8, name="x_bytes_rest")
+        scale_all = const.tile([P, D], F32, name="scale_all")
+        w_rows = const.tile([P, PACK, D], BF16, name="w_rows")
+        bg_rows = const.tile([P, P], BF16, name="bg_rows")
+        cos_sin = []
+        for gi in range(GROUPS):
+            cos_sin_g = per_group.tile([P, TILES * P], BF16, name="cos_sin", tag="cos_sin")
+            cos_sin.append(cos_sin_g)
+        nc.vector.memset(bg_rows[:], 0.0)
+
+        nc.sync.dma_start(out=x_bytes_0[:], in_=x_first[0])
+        nc.scalar.dma_start(out=scale_all[:], in_=x_scale.rearrange("a b k -> (a b k)").partition_broadcast(P))
+        nc.sync.dma_start(out=w_rows[:], in_=w.rearrange("(p t) n -> p t n", t=PACK))
+        nc.sync.dma_start(out=x_bytes_rest[:], in_=x_by_partition[:, 1:GROUPS, :])
+        nc.sync.dma_start(out=bg_rows[0:HEADS, :], in_=b.rearrange("(h p) -> h p", p=P))
+        nc.sync.dma_start(out=bg_rows[HEADS : 2 * HEADS, :], in_=g.rearrange("(h p) -> h p", p=P))
+        for gi in range(GROUPS):
+            for hw in range(4):
+                nc.sync.dma_start(out=cos_sin[gi][hw : P : 4, :], in_=freqs_by_window[gi, hw // 2, hw % 2])
+
+        def bytes_of(gi, q):
+            cols = slice(q * D, (q + 1) * D)
+            if gi == 0:
+                return x_bytes_0[:, cols]
+            return x_bytes_rest[:, gi - 1, cols]
+
+        ones = const.tile([P, 32], F32, name="ones", align_bytes=64)
+        nc.vector.memset(ones[:], 1.0)
+        table_warm = const.tile([P, 1], F32, name="table_warm")
+        nc.scalar.activation(out=table_warm[:], in_=ones[:, 0:1], func=ACT.Sqrt)
+        column_no = const.tile([P, 32], F32, name="column_no", align_bytes=64)
+        nc.vector.tensor_tensor_scan(
+            out=column_no[:], data0=ones[:], data1=ones[:], initial=0.0, op0=ALU.mult, op1=ALU.add
+        )
+        partition_no = const.tile([P, 32], F32, name="partition_no", align_bytes=64)
+        nc.vector.transpose(out=partition_no[:], in_=column_no[:])
+        identity = const.tile([P, P], F32, name="identity")
+        nc.vector.memset(identity[:], 0.0)
+        for blk in range(4):
+            rows = slice(blk * 32, (blk + 1) * 32)
+            nc.vector.tensor_tensor(
+                out=identity[rows, rows], in0=column_no[rows, :], in1=partition_no[rows, :], op=ALU.is_equal
+            )
+        token_perm = const.tile([P, P], F32, name="token_perm")
+        from_v = identity[:].rearrange("p (fi ho hi wo) -> p ho fi hi wo", fi=8, ho=2, hi=4, wo=2)
+        to_v = token_perm[:].rearrange("p (fi hi ho wo) -> p ho fi hi wo", fi=8, ho=2, hi=4, wo=2)
+        for ho in range(2):
+            nc.vector.tensor_copy(out=to_v[:, ho], in_=from_v[:, ho])
+        identity_bf = const.tile([P, P], BF16, name="identity_bf")
+        nc.vector.tensor_copy(out=identity_bf[:], in_=identity[:])
+
+        b_and_g = const.tile([P, 2 * HEADS], F32, name="b_and_g")
+        b_times_g = const.tile([P, HEADS], F32, name="b_times_g")
+        w_grouped = const.tile([P, D, PACK], BF16, name="w_grouped", align_bytes=64)
+        w_codes = const.tile([P, D], U32, name="w_codes", align_bytes=64)
+        w_scales = const.tile([P, D], U8, name="w_scales", align_bytes=64)
+
+        def quantise_w():
+            nc.scalar.copy(out=w_grouped[:], in_=w_rows[:].rearrange("p t n -> p n t"))
+            nc.vector.quantize_mx(
+                out=w_codes[:].bitcast(FP8X4), scales=w_scales[:], in_=w_grouped[:].rearrange("p n t -> p (n t)")
+            )
+
+        def bias_and_gain_to_partitions():
+            turned = psum_a.tile([P, P], BF16, name="turned", tag="a")
+            nc.tensor.transpose(out=turned[:], in_=bg_rows[:], identity=identity_bf[:])
+            nc.vector.tensor_copy(out=b_and_g[:], in_=turned[:, 0 : 2 * HEADS])
+            nc.vector.tensor_tensor(
+                out=b_times_g[:], in0=b_and_g[:, 0:HEADS], in1=b_and_g[:, HEADS : 2 * HEADS], op=ALU.mult
+            )
+
+        x_codes = []
+        x_scales = []
+        gained = []
+        inv_rms = []
+        msin_cos = []
+
+        def stage_a(gi):
+            x_bf = per_group.tile([P, TILES * D], BF16, name="x_bf", tag="x_bf", align_bytes=64)
+            x_grouped = per_group.tile([P, TILES * D], BF16, name="x_grouped", tag="x_grouped", align_bytes=64)
+            grouped_words = x_grouped[:].bitcast(F32)
+            for half in range(2):
+                turned = psum_a.tile([P, D], F32, name="turned", tag="a")
+                for q2 in range(2):
+                    q = half * 2 + q2
+                    cols = slice(q * D, (q + 1) * D)
+                    nc.vector.tensor_tensor(
+                        out=x_bf[:, cols], in0=bytes_of(gi, q).bitcast(FP8), in1=scale_all[:], op=ALU.mult
+                    )
+                    words = x_bf[:, cols].bitcast(F32)
+                    for u in range(2):
+                        c0 = (q2 * 2 + u) * P
+                        nc.tensor.transpose(
+                            out=turned[:, c0 : c0 + P], in_=words[:, u : D // 2 : 2], identity=token_perm[:]
+                        )
+                nc.scalar.copy(
+                    out=grouped_words[:, half * D : (half + 1) * D].rearrange("p (q n u) -> p q n u", q=2, u=2),
+                    in_=turned[:].rearrange("p (q u n) -> p q n u", q=2, u=2),
+                )
+            codes = per_group.tile([P, D], U32, name="x_codes", tag="x_codes", align_bytes=64)
+            scales = per_group.tile([P, D], U8, name="x_scales", tag="x_scales", align_bytes=64)
+            nc.vector.quantize_mx(out=codes[:].bitcast(FP8X4), scales=scales[:], in_=x_grouped[:])
+            x_codes.append(codes)
+            x_scales.append(scales)
+
+        def stage_b(gi):
+            gained_g = []
+            squares = []
+            for h in range(HEADS):
+                head = slice(h * P, (h + 1) * P)
+                acc = psum_acc.tile([P, D], F32, name="acc", tag="acc")
+                for rep in range(MX_REPEATS):
+                    nc.tensor.matmul_mx(
+                        out=acc[:],
+                        lhsT=w_codes[:, head].bitcast(FP8X4),
+                        lhsT_scale=w_scales[:, head],
+                        rhs=x_codes[gi][:].bitcast(FP8X4),
+                        rhs_scale=x_scales[gi][:],
+                        start=True,
+                        stop=True,
+                    )
+                square = per_head.tile([P, D], F32, name="square", tag="square")
+                nc.scalar.activation(out=square[:], in_=acc[:], func=ACT.Square, bias=b_and_g[:, h : h + 1], scale=1.0)
+                gained_h = per_head.tile([P, D], F32, name="gained", tag="gained")
+                nc.scalar.activation(
+                    out=gained_h[:],
+                    in_=acc[:],
+                    func=ACT.Identity,
+                    bias=b_times_g[:, h : h + 1],
+                    scale=b_and_g[:, HEADS + h : HEADS + h + 1],
+                )
+                gained_g.append(gained_h)
+                squares.append(square)
+            gained.append(gained_g)
+            square_sums = psum_sq.tile([P, D], F32, name="square_sums", tag="square_sums")
+            for q in range(TILES):
+                for h in range(HEADS):
+                    nc.tensor.matmul(
+                        out=square_sums[:, q * P : (q + 1) * P],
+                        lhsT=squares[h][:, q * P : (q + 1) * P],
+                        rhs=identity[:],
+                        is_transpose=True,
+                        start=(h == 0),
+                        stop=(h == HEADS - 1),
+                    )
+            total = per_group.tile([P, TILES], F32, name="total", tag="total")
+            nc.vector.tensor_reduce(
+                out=total[:], in_=square_sums[:].rearrange("p (q c) -> p q c", q=TILES), axis=AX.X, op=ALU.add
+            )
+            rms = per_group.tile([P, TILES], F32, name="rms", tag="rms")
+            nc.scalar.activation(out=rms[:], in_=total[:], func=ACT.Sqrt, bias=EPS, scale=1.0 / D)
+            inv_rms_g = per_group.tile([P, TILES], F32, name="inv_rms", tag="inv_rms")
+            nc.vector.reciprocal(out=inv_rms_g[:], in_=rms[:])
+            inv_rms.append(inv_rms_g)
+
+            msin_cos_g = per_group.tile([P, TILES * P], BF16, name="msin_cos", tag="msin_cos")
+            minus_sin = per_group.tile([P, TILES * PAIRS], I32, name="minus_sin", tag="minus_sin")
+            cos_sin_words = cos_sin[gi][:].bitcast(I32)
+            nc.vector.tensor_scalar(
+                out=minus_sin[:],
+                in0=cos_sin_words,
+                scalar1=16,
+                scalar2=0x8000,
+                op0=ALU.logical_shift_right,
+                op1=ALU.bitwise_xor,
+            )
+            nc.vector.scalar_tensor_tensor(
+                out=msin_cos_g[:].bitcast(I32),
+                in0=cos_sin_words,
+                scalar=16,
+                in1=minus_sin[:],
+                op0=ALU.logical_shift_left,
+                op1=ALU.bitwise_or,
+            )
+            msin_cos.append(msin_cos_g)
+
+        def stage_c(gi):
+            by_pair = [P, HEADS, PAIRS, 2]
+            for q in range(TILES):
+                if q % 2 == 0:
+                    y_tokens = psum_c.tile([P, D], F32, name="y_tokens", tag="c")
+                else:
+                    y_tokens = psum_a.tile([P, D], F32, name="y_tokens_a", tag="a")
+                for h in range(HEADS):
+                    nc.tensor.transpose(
+                        out=y_tokens[:, h * P : (h + 1) * P], in_=gained[gi][h][:, q * P : (q + 1) * P], identity=identity[:]
+                    )
+                pairs = y_tokens[:].rearrange("p (h j e) -> p h j e", h=HEADS, e=2)
+                products = []
+                for e, table in ((0, cos_sin[gi]), (1, msin_cos[gi])):
+                    product = per_tile.tile([P, D], F32, name="product%d" % e, tag="product%d" % e)
+                    nc.vector.scalar_tensor_tensor(
+                        out=product[:].rearrange("p (h j f) -> p h j f", h=HEADS, f=2),
+                        in0=pairs[:, :, :, e : e + 1].to_broadcast(by_pair),
+                        scalar=inv_rms[gi][:, q : q + 1],
+                        in1=table[:, q * P : (q + 1) * P].rearrange("p (o j f) -> p o j f", o=1, f=2).to_broadcast(by_pair),
+                        op0=ALU.mult,
+                        op1=ALU.mult,
+                    )
+                    products.append(product)
+                rotated = per_tile.tile([P, D], F32, name="rotated", tag="rotated")
+                last = gi == GROUPS - 1 and q == TILES - 1
+                adder = nc.vector if last else nc.gpsimd
+                adder.tensor_tensor(out=rotated[:], in0=products[0][:], in1=products[1][:], op=ALU.add)
+                nc.sync.dma_start(out=out_by_tile[gi, q], in_=rotated[:])
+
+        for gi in range(A_LEAD):
+            stage_a(gi)
+            if gi == 0:
+                quantise_w()
+                bias_and_gain_to_partitions()
+        for step in range(GROUPS + C_LAG):
+            if step >= C_LAG:
+                stage_c(step - C_LAG)
+            if step < GROUPS:
+                stage_b(step)
+            if step + A_LEAD < GROUPS:
+                stage_a(step + A_LEAD)

@@ -26,7 +26,6 @@ FLOPS = 2 * TOKENS * D * D
 
 A_LEAD = 3
 C_LAG = 2
-MX_REPEATS = 2
 
 
 def tile_selfattention_pa_kernel(tc, x_bytes, x_scale, freqs, w, b, g, out):
@@ -78,7 +77,7 @@ def tile_selfattention_pa_kernel(tc, x_bytes, x_scale, freqs, w, b, g, out):
         ones = const.tile([P, 32], F32, name="ones", align_bytes=64)
         nc.vector.memset(ones[:], 1.0)
         table_warm = const.tile([P, 1], F32, name="table_warm")
-        nc.scalar.activation(out=table_warm[:], in_=ones[:, 0:1], func=ACT.Sqrt)
+        nc.scalar.activation(out=table_warm[:], in_=ones[:, 0:1], func=ACT.Abs_reciprocal_sqrt)
         column_no = const.tile([P, 32], F32, name="column_no", align_bytes=64)
         nc.vector.tensor_tensor_scan(
             out=column_no[:], data0=ones[:], data1=ones[:], initial=0.0, op0=ALU.mult, op1=ALU.add
@@ -160,16 +159,15 @@ def tile_selfattention_pa_kernel(tc, x_bytes, x_scale, freqs, w, b, g, out):
             for h in range(HEADS):
                 head = slice(h * P, (h + 1) * P)
                 acc = psum_acc.tile([P, D], F32, name="acc", tag="acc")
-                for rep in range(MX_REPEATS):
-                    nc.tensor.matmul_mx(
-                        out=acc[:],
-                        lhsT=w_codes[:, head].bitcast(FP8X4),
-                        lhsT_scale=w_scales[:, head],
-                        rhs=x_codes[gi][:].bitcast(FP8X4),
-                        rhs_scale=x_scales[gi][:],
-                        start=True,
-                        stop=True,
-                    )
+                nc.tensor.matmul_mx(
+                    out=acc[:],
+                    lhsT=w_codes[:, head].bitcast(FP8X4),
+                    lhsT_scale=w_scales[:, head],
+                    rhs=x_codes[gi][:].bitcast(FP8X4),
+                    rhs_scale=x_scales[gi][:],
+                    start=True,
+                    stop=True,
+                )
                 square = per_head.tile([P, D], F32, name="square", tag="square")
                 nc.scalar.activation(out=square[:], in_=acc[:], func=ACT.Square, bias=b_and_g[:, h : h + 1], scale=1.0)
                 gained_h = per_head.tile([P, D], F32, name="gained", tag="gained")
@@ -198,10 +196,8 @@ def tile_selfattention_pa_kernel(tc, x_bytes, x_scale, freqs, w, b, g, out):
             nc.vector.tensor_reduce(
                 out=total[:], in_=square_sums[:].rearrange("p (q c) -> p q c", q=TILES), axis=AX.X, op=ALU.add
             )
-            rms = per_group.tile([P, TILES], F32, name="rms", tag="rms")
-            nc.scalar.activation(out=rms[:], in_=total[:], func=ACT.Sqrt, bias=EPS, scale=1.0 / D)
             inv_rms_g = per_group.tile([P, TILES], F32, name="inv_rms", tag="inv_rms")
-            nc.vector.reciprocal(out=inv_rms_g[:], in_=rms[:])
+            nc.scalar.activation(out=inv_rms_g[:], in_=total[:], func=ACT.Abs_reciprocal_sqrt, bias=EPS, scale=1.0 / D)
             inv_rms.append(inv_rms_g)
 
             msin_cos_g = per_group.tile([P, TILES * P], BF16, name="msin_cos", tag="msin_cos")

@@ -11,7 +11,6 @@ FP8 = mybir.dt.float8_e4m3fn
 FP8X4 = mybir.dt.float8_e4m3fn_x4
 ALU = mybir.AluOpType
 ACT = mybir.ActivationFunctionType
-AX = mybir.AxisListType
 
 P = 128
 TOKENS = 2560
@@ -193,9 +192,11 @@ def tile_selfattention_pa_kernel(tc, x_bytes, x_scale, freqs, w, b, g, out):
                         stop=(h == HEADS - 1),
                     )
             total = per_group.tile([P, TILES], F32, name="total", tag="total")
-            nc.vector.tensor_reduce(
-                out=total[:], in_=square_sums[:].rearrange("p (q c) -> p q c", q=TILES), axis=AX.X, op=ALU.add
-            )
+            for q in range(TILES):
+                unused = per_tile.tile([P, P], F32, name="unused", tag="unused")
+                nc.scalar.activation(
+                    out=unused[:], in_=square_sums[:, q * P : (q + 1) * P], func=ACT.Copy, accum_out=total[:, q : q + 1]
+                )
             inv_rms_g = per_group.tile([P, TILES], F32, name="inv_rms", tag="inv_rms")
             nc.scalar.activation(out=inv_rms_g[:], in_=total[:], func=ACT.Abs_reciprocal_sqrt, bias=EPS, scale=1.0 / D)
             inv_rms.append(inv_rms_g)

@@ -25,6 +25,7 @@ FLOPS = 2 * TOKENS * D * D
 
 A_LEAD = 3
 C_LAG = 2
+UNITS = [(gi, 0, TILES) for gi in range(GROUPS - 1)] + [(GROUPS - 1, 0, 2), (GROUPS - 1, 2, 2)]
 
 
 def tile_selfattention_pa_kernel(tc, x_bytes, x_scale, freqs, w, b, g, out):
@@ -39,8 +40,9 @@ def tile_selfattention_pa_kernel(tc, x_bytes, x_scale, freqs, w, b, g, out):
     with ExitStack() as ctx:
         const = ctx.enter_context(tc.tile_pool(name="const", bufs=1))
         per_group = ctx.enter_context(tc.tile_pool(name="per_group", bufs=GROUPS))
+        per_unit = ctx.enter_context(tc.tile_pool(name="per_unit", bufs=len(UNITS)))
         per_head = ctx.enter_context(tc.tile_pool(name="per_head", bufs=4 * HEADS))
-        per_tile = ctx.enter_context(tc.tile_pool(name="per_tile", bufs=6))
+        per_tile = ctx.enter_context(tc.tile_pool(name="per_tile", bufs=4))
         psum_a = ctx.enter_context(tc.psum_pool(name="psum_a", bufs=2))
         psum_acc = ctx.enter_context(tc.psum_pool(name="psum_acc", bufs=2))
         psum_sq = ctx.enter_context(tc.psum_pool(name="psum_sq", bufs=2))
@@ -120,9 +122,9 @@ def tile_selfattention_pa_kernel(tc, x_bytes, x_scale, freqs, w, b, g, out):
 
         x_codes = []
         x_scales = []
-        gained = []
-        inv_rms = []
-        msin_cos = []
+        gained = {}
+        inv_rms = {}
+        cos_msin = []
 
         def stage_a(gi):
             x_bf = per_group.tile([P, TILES * D], BF16, name="x_bf", tag="x_bf", align_bytes=64)
@@ -152,24 +154,38 @@ def tile_selfattention_pa_kernel(tc, x_bytes, x_scale, freqs, w, b, g, out):
             x_codes.append(codes)
             x_scales.append(scales)
 
-        def stage_b(gi):
-            gained_g = []
+        def second_table(gi):
+            cos_msin_g = per_group.tile([P, TILES * P], BF16, name="cos_msin", tag="cos_msin")
+            nc.vector.tensor_scalar(
+                out=cos_msin_g[:].bitcast(I32),
+                in0=cos_sin[gi][:].bitcast(I32),
+                scalar1=-0x80000000,
+                scalar2=None,
+                op0=ALU.bitwise_xor,
+            )
+            cos_msin.append(cos_msin_g)
+
+        def stage_b(unit):
+            gi, first, count = unit
+            tokens = slice(first * P, (first + count) * P)
+            width = count * P
+            gained_u = []
             squares = []
             for h in range(HEADS):
                 head = slice(h * P, (h + 1) * P)
-                acc = psum_acc.tile([P, D], F32, name="acc", tag="acc")
+                acc = psum_acc.tile([P, width], F32, name="acc", tag="acc")
                 nc.tensor.matmul_mx(
                     out=acc[:],
                     lhsT=w_codes[:, head].bitcast(FP8X4),
                     lhsT_scale=w_scales[:, head],
-                    rhs=x_codes[gi][:].bitcast(FP8X4),
-                    rhs_scale=x_scales[gi][:],
+                    rhs=x_codes[gi][:, tokens].bitcast(FP8X4),
+                    rhs_scale=x_scales[gi][:, tokens],
                     start=True,
                     stop=True,
                 )
-                square = per_head.tile([P, D], F32, name="square", tag="square")
+                square = per_head.tile([P, width], F32, name="square", tag="square")
                 nc.scalar.activation(out=square[:], in_=acc[:], func=ACT.Square, bias=b_and_g[:, h : h + 1], scale=1.0)
-                gained_h = per_head.tile([P, D], F32, name="gained", tag="gained")
+                gained_h = per_head.tile([P, width], F32, name="gained", tag="gained")
                 nc.scalar.activation(
                     out=gained_h[:],
                     in_=acc[:],
@@ -177,90 +193,82 @@ def tile_selfattention_pa_kernel(tc, x_bytes, x_scale, freqs, w, b, g, out):
                     bias=b_times_g[:, h : h + 1],
                     scale=b_and_g[:, HEADS + h : HEADS + h + 1],
                 )
-                gained_g.append(gained_h)
+                gained_u.append(gained_h)
                 squares.append(square)
-            gained.append(gained_g)
-            square_sums = psum_sq.tile([P, D], F32, name="square_sums", tag="square_sums")
-            for q in range(TILES):
+            gained[unit] = gained_u
+            square_sums = psum_sq.tile([P, width], F32, name="square_sums", tag="square_sums")
+            for i in range(count):
                 for h in range(HEADS):
                     nc.tensor.matmul(
-                        out=square_sums[:, q * P : (q + 1) * P],
-                        lhsT=squares[h][:, q * P : (q + 1) * P],
+                        out=square_sums[:, i * P : (i + 1) * P],
+                        lhsT=squares[h][:, i * P : (i + 1) * P],
                         rhs=identity[:],
                         is_transpose=True,
                         start=(h == 0),
                         stop=(h == HEADS - 1),
                     )
-            total = per_group.tile([P, TILES], F32, name="total", tag="total")
-            for q in range(TILES):
+            total = per_unit.tile([P, count], F32, name="total", tag="total")
+            for i in range(count):
                 unused = per_tile.tile([P, P], F32, name="unused", tag="unused")
                 nc.scalar.activation(
-                    out=unused[:], in_=square_sums[:, q * P : (q + 1) * P], func=ACT.Copy, accum_out=total[:, q : q + 1]
+                    out=unused[:], in_=square_sums[:, i * P : (i + 1) * P], func=ACT.Copy, accum_out=total[:, i : i + 1]
                 )
-            inv_rms_g = per_group.tile([P, TILES], F32, name="inv_rms", tag="inv_rms")
-            nc.scalar.activation(out=inv_rms_g[:], in_=total[:], func=ACT.Abs_reciprocal_sqrt, bias=EPS, scale=1.0 / D)
-            inv_rms.append(inv_rms_g)
+            inv_rms_u = per_unit.tile([P, count], F32, name="inv_rms", tag="inv_rms")
+            nc.scalar.activation(out=inv_rms_u[:], in_=total[:], func=ACT.Abs_reciprocal_sqrt, bias=EPS, scale=1.0 / D)
+            inv_rms[unit] = inv_rms_u
 
-            msin_cos_g = per_group.tile([P, TILES * P], BF16, name="msin_cos", tag="msin_cos")
-            minus_sin = per_group.tile([P, TILES * PAIRS], I32, name="minus_sin", tag="minus_sin")
-            cos_sin_words = cos_sin[gi][:].bitcast(I32)
-            nc.vector.tensor_scalar(
-                out=minus_sin[:],
-                in0=cos_sin_words,
-                scalar1=16,
-                scalar2=0x8000,
-                op0=ALU.logical_shift_right,
-                op1=ALU.bitwise_xor,
-            )
-            nc.vector.scalar_tensor_tensor(
-                out=msin_cos_g[:].bitcast(I32),
-                in0=cos_sin_words,
-                scalar=16,
-                in1=minus_sin[:],
-                op0=ALU.logical_shift_left,
-                op1=ALU.bitwise_or,
-            )
-            msin_cos.append(msin_cos_g)
-
-        def stage_c(gi):
+        def stage_c(unit):
+            gi, first, count = unit
             by_pair = [P, HEADS, PAIRS, 2]
-            for q in range(TILES):
-                if q % 2 == 0:
-                    y_tokens = psum_c.tile([P, D], F32, name="y_tokens", tag="c")
-                else:
-                    y_tokens = psum_a.tile([P, D], F32, name="y_tokens_a", tag="a")
-                for h in range(HEADS):
-                    nc.tensor.transpose(
-                        out=y_tokens[:, h * P : (h + 1) * P], in_=gained[gi][h][:, q * P : (q + 1) * P], identity=identity[:]
-                    )
-                pairs = y_tokens[:].rearrange("p (h j e) -> p h j e", h=HEADS, e=2)
+            for start in range(0, count, 2):
                 products = []
-                for e, table in ((0, cos_sin[gi]), (1, msin_cos[gi])):
-                    product = per_tile.tile([P, D], F32, name="product%d" % e, tag="product%d" % e)
-                    nc.vector.scalar_tensor_tensor(
-                        out=product[:].rearrange("p (h j f) -> p h j f", h=HEADS, f=2),
-                        in0=pairs[:, :, :, e : e + 1].to_broadcast(by_pair),
-                        scalar=inv_rms[gi][:, q : q + 1],
-                        in1=table[:, q * P : (q + 1) * P].rearrange("p (o j f) -> p o j f", o=1, f=2).to_broadcast(by_pair),
-                        op0=ALU.mult,
-                        op1=ALU.mult,
-                    )
+                for e in range(2):
+                    product = per_tile.tile([P, 2, D], F32, name="product%d" % e, tag="product%d" % e)
                     products.append(product)
-                rotated = per_tile.tile([P, D], F32, name="rotated", tag="rotated")
-                last = gi == GROUPS - 1 and q == TILES - 1
-                adder = nc.vector if last else nc.gpsimd
-                adder.tensor_tensor(out=rotated[:], in0=products[0][:], in1=products[1][:], op=ALU.add)
-                nc.sync.dma_start(out=out_by_tile[gi, q], in_=rotated[:])
+                rotated = per_tile.tile([P, 2, D], F32, name="rotated", tag="rotated")
+                for i in range(2):
+                    q = first + start + i
+                    if i == 0:
+                        y_tokens = psum_c.tile([P, D], F32, name="y_tokens", tag="c")
+                    else:
+                        y_tokens = psum_a.tile([P, D], F32, name="y_tokens_a", tag="a")
+                    for h in range(HEADS):
+                        nc.tensor.transpose(
+                            out=y_tokens[:, h * P : (h + 1) * P],
+                            in_=gained[unit][h][:, (start + i) * P : (start + i + 1) * P],
+                            identity=identity[:],
+                        )
+                    pairs = y_tokens[:].rearrange("p (h j e) -> p h j e", h=HEADS, e=2)
+                    for e, table, step in ((0, cos_sin[gi], 1), (1, cos_msin[gi], -1)):
+                        nc.vector.scalar_tensor_tensor(
+                            out=products[e][:, i, :].rearrange("p (h j f) -> p h j f", h=HEADS, f=2)[:, :, :, ::step],
+                            in0=pairs[:, :, :, e : e + 1].to_broadcast(by_pair),
+                            scalar=inv_rms[unit][:, start + i : start + i + 1],
+                            in1=table[:, q * P : (q + 1) * P].rearrange("p (o j f) -> p o j f", o=1, f=2).to_broadcast(by_pair),
+                            op0=ALU.mult,
+                            op1=ALU.mult,
+                        )
+                if unit == UNITS[-1]:
+                    for i in range(2):
+                        nc.vector.tensor_tensor(
+                            out=rotated[:, i, :], in0=products[0][:, i, :], in1=products[1][:, i, :], op=ALU.add
+                        )
+                else:
+                    nc.gpsimd.tensor_tensor(out=rotated[:], in0=products[0][:], in1=products[1][:], op=ALU.add)
+                for i in range(2):
+                    nc.sync.dma_start(out=out_by_tile[gi, first + start + i], in_=rotated[:, i, :])
 
         for gi in range(A_LEAD):
             stage_a(gi)
             if gi == 0:
                 quantise_w()
                 bias_and_gain_to_partitions()
-        for step in range(GROUPS + C_LAG):
+        for step in range(len(UNITS) + C_LAG):
             if step >= C_LAG:
-                stage_c(step - C_LAG)
-            if step < GROUPS:
-                stage_b(step)
+                stage_c(UNITS[step - C_LAG])
+            if step < len(UNITS):
+                stage_b(UNITS[step])
+                if UNITS[step][1] == 0:
+                    second_table(UNITS[step][0])
             if step + A_LEAD < GROUPS:
                 stage_a(step + A_LEAD)

@@ -43,10 +43,9 @@ def tile_selfattention_pa_kernel(tc, x_bytes, x_scale, freqs, w, b, g, out):
         per_unit = ctx.enter_context(tc.tile_pool(name="per_unit", bufs=len(UNITS)))
         per_head = ctx.enter_context(tc.tile_pool(name="per_head", bufs=4 * HEADS))
         per_tile = ctx.enter_context(tc.tile_pool(name="per_tile", bufs=4))
-        psum_a = ctx.enter_context(tc.psum_pool(name="psum_a", bufs=2))
+        psum_turn = ctx.enter_context(tc.psum_pool(name="psum_turn", bufs=3))
         psum_acc = ctx.enter_context(tc.psum_pool(name="psum_acc", bufs=2))
-        psum_sq = ctx.enter_context(tc.psum_pool(name="psum_sq", bufs=2))
-        psum_c = ctx.enter_context(tc.psum_pool(name="psum_c", bufs=2))
+        psum_sq = ctx.enter_context(tc.psum_pool(name="psum_sq", bufs=1))
 
         x_bytes_0 = const.tile([P, TILES * D], U8, name="x_bytes_0")
         x_bytes_rest = const.tile([P, GROUPS - 1, TILES * D], U8, name="x_bytes_rest")
@@ -113,7 +112,7 @@ def tile_selfattention_pa_kernel(tc, x_bytes, x_scale, freqs, w, b, g, out):
             )
 
         def bias_and_gain_to_partitions():
-            turned = psum_a.tile([P, P], BF16, name="turned", tag="a")
+            turned = psum_turn.tile([P, P], BF16, name="turned", tag="turn")
             nc.tensor.transpose(out=turned[:], in_=bg_rows[:], identity=identity_bf[:])
             nc.vector.tensor_copy(out=b_and_g[:], in_=turned[:, 0 : 2 * HEADS])
             nc.vector.tensor_tensor(
@@ -131,7 +130,7 @@ def tile_selfattention_pa_kernel(tc, x_bytes, x_scale, freqs, w, b, g, out):
             x_grouped = per_group.tile([P, TILES * D], BF16, name="x_grouped", tag="x_grouped", align_bytes=64)
             grouped_words = x_grouped[:].bitcast(F32)
             for half in range(2):
-                turned = psum_a.tile([P, D], F32, name="turned", tag="a")
+                turned = psum_turn.tile([P, D], F32, name="turned", tag="turn")
                 for q2 in range(2):
                     q = half * 2 + q2
                     cols = slice(q * D, (q + 1) * D)
@@ -171,30 +170,34 @@ def tile_selfattention_pa_kernel(tc, x_bytes, x_scale, freqs, w, b, g, out):
             width = count * P
             gained_u = []
             squares = []
-            for h in range(HEADS):
-                head = slice(h * P, (h + 1) * P)
-                acc = psum_acc.tile([P, width], F32, name="acc", tag="acc")
-                nc.tensor.matmul_mx(
-                    out=acc[:],
-                    lhsT=w_codes[:, head].bitcast(FP8X4),
-                    lhsT_scale=w_scales[:, head],
-                    rhs=x_codes[gi][:, tokens].bitcast(FP8X4),
-                    rhs_scale=x_scales[gi][:, tokens],
-                    start=True,
-                    stop=True,
-                )
-                square = per_head.tile([P, width], F32, name="square", tag="square")
-                nc.scalar.activation(out=square[:], in_=acc[:], func=ACT.Square, bias=b_and_g[:, h : h + 1], scale=1.0)
-                gained_h = per_head.tile([P, width], F32, name="gained", tag="gained")
-                nc.scalar.activation(
-                    out=gained_h[:],
-                    in_=acc[:],
-                    func=ACT.Identity,
-                    bias=b_times_g[:, h : h + 1],
-                    scale=b_and_g[:, HEADS + h : HEADS + h + 1],
-                )
-                gained_u.append(gained_h)
-                squares.append(square)
+            for h0 in range(0, HEADS, 2):
+                acc_pair = psum_acc.tile([P, 2, D], F32, name="acc_pair", tag="acc")
+                for i in range(2):
+                    head = slice((h0 + i) * P, (h0 + i + 1) * P)
+                    nc.tensor.matmul_mx(
+                        out=acc_pair[:, i, 0:width],
+                        lhsT=w_codes[:, head].bitcast(FP8X4),
+                        lhsT_scale=w_scales[:, head],
+                        rhs=x_codes[gi][:, tokens].bitcast(FP8X4),
+                        rhs_scale=x_scales[gi][:, tokens],
+                        start=True,
+                        stop=True,
+                    )
+                for i in range(2):
+                    h = h0 + i
+                    acc = acc_pair[:, i, 0:width]
+                    square = per_head.tile([P, width], F32, name="square", tag="square")
+                    nc.scalar.activation(out=square[:], in_=acc, func=ACT.Square, bias=b_and_g[:, h : h + 1], scale=1.0)
+                    gained_h = per_head.tile([P, width], F32, name="gained", tag="gained")
+                    nc.scalar.activation(
+                        out=gained_h[:],
+                        in_=acc,
+                        func=ACT.Identity,
+                        bias=b_times_g[:, h : h + 1],
+                        scale=b_and_g[:, HEADS + h : HEADS + h + 1],
+                    )
+                    gained_u.append(gained_h)
+                    squares.append(square)
             gained[unit] = gained_u
             square_sums = psum_sq.tile([P, width], F32, name="square_sums", tag="square_sums")
             for i in range(count):
@@ -228,10 +231,7 @@ def tile_selfattention_pa_kernel(tc, x_bytes, x_scale, freqs, w, b, g, out):
                 rotated = per_tile.tile([P, 2, D], F32, name="rotated", tag="rotated")
                 for i in range(2):
                     q = first + start + i
-                    if i == 0:
-                        y_tokens = psum_c.tile([P, D], F32, name="y_tokens", tag="c")
-                    else:
-                        y_tokens = psum_a.tile([P, D], F32, name="y_tokens_a", tag="a")
+                    y_tokens = psum_turn.tile([P, D], F32, name="y_tokens", tag="turn")
                     for h in range(HEADS):
                         nc.tensor.transpose(
                             out=y_tokens[:, h * P : (h + 1) * P],

@@ -30,8 +30,7 @@ UNITS = [(gi, 0, TILES) for gi in range(GROUPS - 1)] + [(GROUPS - 1, 0, 2), (GRO
 
 def tile_selfattention_pa_kernel(tc, x_bytes, x_scale, freqs, w, b, g, out):
     nc = tc.nc
-    x_first = x_bytes.rearrange("o (g p q) k -> (o g) p (q k)", p=P, q=TILES)
-    x_by_partition = x_bytes.rearrange("o (g p q) k -> p (o g) (q k)", p=P, q=TILES)
+    x_by_group = x_bytes.rearrange("o (g p q) k -> (o g) p (q k)", p=P, q=TILES)
     freqs_by_window = freqs.rearrange(
         "(g fi ho hi wo q) o j f -> g ho wo fi hi (q o j f)", g=GROUPS, fi=8, ho=2, hi=4, wo=2, q=TILES
     )
@@ -47,8 +46,7 @@ def tile_selfattention_pa_kernel(tc, x_bytes, x_scale, freqs, w, b, g, out):
         psum_acc = ctx.enter_context(tc.psum_pool(name="psum_acc", bufs=2))
         psum_sq = ctx.enter_context(tc.psum_pool(name="psum_sq", bufs=1))
 
-        x_bytes_0 = const.tile([P, TILES * D], U8, name="x_bytes_0")
-        x_bytes_rest = const.tile([P, GROUPS - 1, TILES * D], U8, name="x_bytes_rest")
+        x_bytes_sb = const.tile([P, GROUPS, TILES * D], U8, name="x_bytes_sb")
         scale_all = const.tile([P, D], F32, name="scale_all")
         w_rows = const.tile([P, PACK, D], BF16, name="w_rows")
         bg_rows = const.tile([P, P], BF16, name="bg_rows")
@@ -58,21 +56,20 @@ def tile_selfattention_pa_kernel(tc, x_bytes, x_scale, freqs, w, b, g, out):
             cos_sin.append(cos_sin_g)
         nc.vector.memset(bg_rows[:], 0.0)
 
-        nc.sync.dma_start(out=x_bytes_0[:], in_=x_first[0])
+        def load_x(gi):
+            nc.sync.dma_start(out=x_bytes_sb[:, gi, :], in_=x_by_group[gi])
+
+        load_x(0)
         nc.scalar.dma_start(out=scale_all[:], in_=x_scale.rearrange("a b k -> (a b k)").partition_broadcast(P))
+        load_x(1)
         nc.sync.dma_start(out=w_rows[:], in_=w.rearrange("(p t) n -> p t n", t=PACK))
-        nc.sync.dma_start(out=x_bytes_rest[:], in_=x_by_partition[:, 1:GROUPS, :])
         nc.sync.dma_start(out=bg_rows[0:HEADS, :], in_=b.rearrange("(h p) -> h p", p=P))
         nc.sync.dma_start(out=bg_rows[HEADS : 2 * HEADS, :], in_=g.rearrange("(h p) -> h p", p=P))
+        for gi in range(2, GROUPS):
+            load_x(gi)
         for gi in range(GROUPS):
             for hw in range(4):
                 nc.sync.dma_start(out=cos_sin[gi][hw : P : 4, :], in_=freqs_by_window[gi, hw // 2, hw % 2])
-
-        def bytes_of(gi, q):
-            cols = slice(q * D, (q + 1) * D)
-            if gi == 0:
-                return x_bytes_0[:, cols]
-            return x_bytes_rest[:, gi - 1, cols]
 
         ones = const.tile([P, 32], F32, name="ones", align_bytes=64)
         nc.vector.memset(ones[:], 1.0)
@@ -135,7 +132,7 @@ def tile_selfattention_pa_kernel(tc, x_bytes, x_scale, freqs, w, b, g, out):
                     q = half * 2 + q2
                     cols = slice(q * D, (q + 1) * D)
                     nc.vector.tensor_tensor(
-                        out=x_bf[:, cols], in0=bytes_of(gi, q).bitcast(FP8), in1=scale_all[:], op=ALU.mult
+                        out=x_bf[:, cols], in0=x_bytes_sb[:, gi, cols].bitcast(FP8), in1=scale_all[:], op=ALU.mult
                     )
                     words = x_bf[:, cols].bitcast(F32)
                     for u in range(2):

@@ -25,6 +25,7 @@ FLOPS = 2 * TOKENS * D * D
 
 A_LEAD = 3
 C_LAG = 2
+WIDE_FROM = 2
 UNITS = [(gi, 0, TILES) for gi in range(GROUPS - 1)] + [(GROUPS - 1, 0, 2), (GROUPS - 1, 2, 2)]
 
 
@@ -47,7 +48,7 @@ def tile_selfattention_pa_kernel(tc, x_bytes, x_scale, freqs, w, b, g, out):
         psum_sq = ctx.enter_context(tc.psum_pool(name="psum_sq", bufs=1))
 
         x_bytes_sb = const.tile([P, GROUPS, TILES * D], U8, name="x_bytes_sb")
-        scale_all = const.tile([P, D], F32, name="scale_all")
+        scale_all = const.tile([P, 2, D], F32, name="scale_all")
         w_rows = const.tile([P, PACK, D], BF16, name="w_rows")
         bg_rows = const.tile([P, P], BF16, name="bg_rows")
         cos_sin = []
@@ -60,9 +61,9 @@ def tile_selfattention_pa_kernel(tc, x_bytes, x_scale, freqs, w, b, g, out):
             nc.sync.dma_start(out=x_bytes_sb[:, gi, :], in_=x_by_group[gi])
 
         load_x(0)
-        nc.scalar.dma_start(out=scale_all[:], in_=x_scale.rearrange("a b k -> (a b k)").partition_broadcast(P))
-        load_x(1)
+        nc.scalar.dma_start(out=scale_all[:, 0, :], in_=x_scale.rearrange("a b k -> (a b k)").partition_broadcast(P))
         nc.sync.dma_start(out=w_rows[:], in_=w.rearrange("(p t) n -> p t n", t=PACK))
+        load_x(1)
         nc.sync.dma_start(out=bg_rows[0:HEADS, :], in_=b.rearrange("(h p) -> h p", p=P))
         nc.sync.dma_start(out=bg_rows[HEADS : 2 * HEADS, :], in_=g.rearrange("(h p) -> h p", p=P))
         for gi in range(2, GROUPS):
@@ -75,6 +76,7 @@ def tile_selfattention_pa_kernel(tc, x_bytes, x_scale, freqs, w, b, g, out):
         nc.vector.memset(ones[:], 1.0)
         table_warm = const.tile([P, 1], F32, name="table_warm")
         nc.scalar.activation(out=table_warm[:], in_=ones[:, 0:1], func=ACT.Abs_reciprocal_sqrt)
+        nc.scalar.copy(out=scale_all[:, 1, :], in_=scale_all[:, 0, :])
         column_no = const.tile([P, 32], F32, name="column_no", align_bytes=64)
         nc.vector.tensor_tensor_scan(
             out=column_no[:], data0=ones[:], data1=ones[:], initial=0.0, op0=ALU.mult, op1=ALU.add
@@ -103,7 +105,9 @@ def tile_selfattention_pa_kernel(tc, x_bytes, x_scale, freqs, w, b, g, out):
         w_scales = const.tile([P, D], U8, name="w_scales", align_bytes=64)
 
         def quantise_w():
-            nc.scalar.copy(out=w_grouped[:], in_=w_rows[:].rearrange("p t n -> p n t"))
+            nc.scalar.copy(
+                out=w_grouped[:].rearrange("p (c i) t -> p c t i", i=4), in_=w_rows[:].rearrange("p t (c i) -> p c t i", i=4)
+            )
             nc.vector.quantize_mx(
                 out=w_codes[:].bitcast(FP8X4), scales=w_scales[:], in_=w_grouped[:].rearrange("p n t -> p (n t)")
             )
@@ -128,12 +132,21 @@ def tile_selfattention_pa_kernel(tc, x_bytes, x_scale, freqs, w, b, g, out):
             grouped_words = x_grouped[:].bitcast(F32)
             for half in range(2):
                 turned = psum_turn.tile([P, D], F32, name="turned", tag="turn")
+                if gi >= WIDE_FROM:
+                    both = slice(half * 2 * D, (half + 1) * 2 * D)
+                    nc.vector.tensor_tensor(
+                        out=x_bf[:, both],
+                        in0=x_bytes_sb[:, gi, both].bitcast(FP8),
+                        in1=scale_all[:].rearrange("p c k -> p (c k)"),
+                        op=ALU.mult,
+                    )
                 for q2 in range(2):
                     q = half * 2 + q2
                     cols = slice(q * D, (q + 1) * D)
-                    nc.vector.tensor_tensor(
-                        out=x_bf[:, cols], in0=x_bytes_sb[:, gi, cols].bitcast(FP8), in1=scale_all[:], op=ALU.mult
-                    )
+                    if gi < WIDE_FROM:
+                        nc.vector.tensor_tensor(
+                            out=x_bf[:, cols], in0=x_bytes_sb[:, gi, cols].bitcast(FP8), in1=scale_all[:, 0, :], op=ALU.mult
+                        )
                     words = x_bf[:, cols].bitcast(F32)
                     for u in range(2):
                         c0 = (q2 * 2 + u) * P

@@ -180,7 +180,7 @@ def tile_selfattention_pa_kernel(tc, x_bytes, x_scale, freqs, w, b, g, out):
             width = count * P
             gained_u = []
             squares = []
-            for h0 in range(0, HEADS, 2):
+            def fill(h0):
                 acc_pair = psum_acc.tile([P, 2, D], F32, name="acc_pair", tag="acc")
                 for i in range(2):
                     head = slice((h0 + i) * P, (h0 + i + 1) * P)
@@ -193,21 +193,36 @@ def tile_selfattention_pa_kernel(tc, x_bytes, x_scale, freqs, w, b, g, out):
                         start=True,
                         stop=True,
                     )
-                for i in range(2):
-                    h = h0 + i
-                    acc = acc_pair[:, i, 0:width]
-                    square = per_head.tile([P, width], F32, name="square", tag="square")
-                    nc.scalar.activation(out=square[:], in_=acc, func=ACT.Square, bias=b_and_g[:, h : h + 1], scale=1.0)
-                    gained_h = per_head.tile([P, width], F32, name="gained", tag="gained")
-                    nc.scalar.activation(
-                        out=gained_h[:],
-                        in_=acc,
-                        func=ACT.Identity,
-                        bias=b_times_g[:, h : h + 1],
-                        scale=b_and_g[:, HEADS + h : HEADS + h + 1],
-                    )
-                    gained_u.append(gained_h)
-                    squares.append(square)
+                return [acc_pair[:, 0, 0:width], acc_pair[:, 1, 0:width]]
+
+            def square_of(h, acc):
+                square = per_head.tile([P, width], F32, name="square", tag="square")
+                nc.scalar.activation(out=square[:], in_=acc, func=ACT.Square, bias=b_and_g[:, h : h + 1], scale=1.0)
+                squares.append(square)
+
+            def gain_of(h, acc):
+                gained_h = per_head.tile([P, width], F32, name="gained", tag="gained")
+                nc.scalar.activation(
+                    out=gained_h[:],
+                    in_=acc,
+                    func=ACT.Identity,
+                    bias=b_times_g[:, h : h + 1],
+                    scale=b_and_g[:, HEADS + h : HEADS + h + 1],
+                )
+                gained_u.append(gained_h)
+
+            if unit == UNITS[-1]:
+                accs = fill(0) + fill(2)
+                for h in range(HEADS):
+                    square_of(h, accs[h])
+                for h in range(HEADS):
+                    gain_of(h, accs[h])
+            else:
+                for h0 in range(0, HEADS, 2):
+                    accs = fill(h0)
+                    for i in range(2):
+                        square_of(h0 + i, accs[i])
+                        gain_of(h0 + i, accs[i])
             gained[unit] = gained_u
             square_sums = psum_sq.tile([P, width], F32, name="square_sums", tag="square_sums")
             for i in range(count):

@@ -124,7 +124,7 @@ def tile_selfattention_pa_kernel(tc, x_bytes, x_scale, freqs, w, b, g, out):
         x_scales = []
         gained = {}
         inv_rms = {}
-        cos_msin = []
+        msin_cos = []
 
         def stage_a(gi):
             x_bf = per_group.tile([P, TILES * D], BF16, name="x_bf", tag="x_bf", align_bytes=64)
@@ -164,15 +164,14 @@ def tile_selfattention_pa_kernel(tc, x_bytes, x_scale, freqs, w, b, g, out):
             x_scales.append(scales)
 
         def second_table(gi):
-            cos_msin_g = per_group.tile([P, TILES * P], BF16, name="cos_msin", tag="cos_msin")
-            nc.vector.tensor_scalar(
-                out=cos_msin_g[:].bitcast(I32),
-                in0=cos_sin[gi][:].bitcast(I32),
-                scalar1=-0x80000000,
-                scalar2=None,
-                op0=ALU.bitwise_xor,
-            )
-            cos_msin.append(cos_msin_g)
+            msin_cos_g = per_group.tile([P, TILES * P], BF16, name="msin_cos", tag="msin_cos")
+            from_t = cos_sin[gi][:].rearrange("p (c f) -> p c f", f=2)
+            to_t = msin_cos_g[:].rearrange("p (c f) -> p c f", f=2)
+            for f, factor in ((0, -1.0), (1, 1.0)):
+                nc.gpsimd.tensor_scalar(
+                    out=to_t[:, :, f], in0=from_t[:, :, 1 - f], scalar1=factor, scalar2=0.0, op0=ALU.mult, op1=ALU.add
+                )
+            msin_cos.append(msin_cos_g)
 
         def stage_b(unit):
             gi, first, count = unit
@@ -264,9 +263,9 @@ def tile_selfattention_pa_kernel(tc, x_bytes, x_scale, freqs, w, b, g, out):
                             identity=identity[:],
                         )
                     pairs = y_tokens[:].rearrange("p (h j e) -> p h j e", h=HEADS, e=2)
-                    for e, table, step in ((0, cos_sin[gi], 1), (1, cos_msin[gi], -1)):
+                    for e, table in ((0, cos_sin[gi]), (1, msin_cos[gi])):
                         nc.vector.scalar_tensor_tensor(
-                            out=products[e][:, i, :].rearrange("p (h j f) -> p h j f", h=HEADS, f=2)[:, :, :, ::step],
+                            out=products[e][:, i, :].rearrange("p (h j f) -> p h j f", h=HEADS, f=2),
                             in0=pairs[:, :, :, e : e + 1].to_broadcast(by_pair),
                             scalar=inv_rms[unit][:, start + i : start + i + 1],
                             in1=table[:, q * P : (q + 1) * P].rearrange("p (o j f) -> p o j f", o=1, f=2).to_broadcast(by_pair),
@@ -288,12 +287,12 @@ def tile_selfattention_pa_kernel(tc, x_bytes, x_scale, freqs, w, b, g, out):
             if gi == 0:
                 quantise_w()
                 bias_and_gain_to_partitions()
+        for gi in range(GROUPS):
+            second_table(gi)
         for step in range(len(UNITS) + C_LAG):
             if step >= C_LAG:
                 stage_c(UNITS[step - C_LAG])
             if step < len(UNITS):
                 stage_b(UNITS[step])
-                if UNITS[step][1] == 0:
-                    second_table(UNITS[step][0])
             if step + A_LEAD < GROUPS:
                 stage_a(step + A_LEAD)

@@ -23,11 +23,6 @@ TILES = 4
 EPS = 1e-5
 FLOPS = 2 * TOKENS * D * D
 
-A_LEAD = 3
-C_LAG = 2
-WIDE_FROM = 2
-UNITS = [(gi, 0, TILES) for gi in range(GROUPS - 1)] + [(GROUPS - 1, 0, 2), (GROUPS - 1, 2, 2)]
-
 
 def tile_selfattention_pa_kernel(tc, x_bytes, x_scale, freqs, w, b, g, out):
     nc = tc.nc
@@ -40,15 +35,15 @@ def tile_selfattention_pa_kernel(tc, x_bytes, x_scale, freqs, w, b, g, out):
     with ExitStack() as ctx:
         const = ctx.enter_context(tc.tile_pool(name="const", bufs=1))
         per_group = ctx.enter_context(tc.tile_pool(name="per_group", bufs=GROUPS))
-        per_unit = ctx.enter_context(tc.tile_pool(name="per_unit", bufs=len(UNITS)))
-        per_head = ctx.enter_context(tc.tile_pool(name="per_head", bufs=4 * HEADS))
+        per_head = ctx.enter_context(tc.tile_pool(name="per_head", bufs=3 * HEADS))
         per_tile = ctx.enter_context(tc.tile_pool(name="per_tile", bufs=4))
         psum_turn = ctx.enter_context(tc.psum_pool(name="psum_turn", bufs=3))
         psum_acc = ctx.enter_context(tc.psum_pool(name="psum_acc", bufs=2))
         psum_sq = ctx.enter_context(tc.psum_pool(name="psum_sq", bufs=1))
+        ctx.enter_context(tc.manual_schedule())
 
         x_bytes_sb = const.tile([P, GROUPS, TILES * D], U8, name="x_bytes_sb")
-        scale_all = const.tile([P, 2, D], F32, name="scale_all")
+        scale_cols = const.tile([P, PACK], F32, name="scale_cols")
         w_rows = const.tile([P, PACK, D], BF16, name="w_rows")
         bg_rows = const.tile([P, P], BF16, name="bg_rows")
         cos_sin = []
@@ -61,7 +56,7 @@ def tile_selfattention_pa_kernel(tc, x_bytes, x_scale, freqs, w, b, g, out):
             nc.sync.dma_start(out=x_bytes_sb[:, gi, :], in_=x_by_group[gi])
 
         load_x(0)
-        nc.scalar.dma_start(out=scale_all[:, 0, :], in_=x_scale.rearrange("a b k -> (a b k)").partition_broadcast(P))
+        nc.sync.dma_start(out=scale_cols[:], in_=x_scale.rearrange("a b (p t) -> (a b p) t", t=PACK))
         nc.sync.dma_start(out=w_rows[:], in_=w.rearrange("(p t) n -> p t n", t=PACK))
         load_x(1)
         nc.sync.dma_start(out=bg_rows[0:HEADS, :], in_=b.rearrange("(h p) -> h p", p=P))
@@ -76,7 +71,6 @@ def tile_selfattention_pa_kernel(tc, x_bytes, x_scale, freqs, w, b, g, out):
         nc.vector.memset(ones[:], 1.0)
         table_warm = const.tile([P, 1], F32, name="table_warm")
         nc.scalar.activation(out=table_warm[:], in_=ones[:, 0:1], func=ACT.Abs_reciprocal_sqrt)
-        nc.scalar.copy(out=scale_all[:, 1, :], in_=scale_all[:, 0, :])
         column_no = const.tile([P, 32], F32, name="column_no", align_bytes=64)
         nc.vector.tensor_tensor_scan(
             out=column_no[:], data0=ones[:], data1=ones[:], initial=0.0, op0=ALU.mult, op1=ALU.add
@@ -104,10 +98,12 @@ def tile_selfattention_pa_kernel(tc, x_bytes, x_scale, freqs, w, b, g, out):
         w_codes = const.tile([P, D], U32, name="w_codes", align_bytes=64)
         w_scales = const.tile([P, D], U8, name="w_scales", align_bytes=64)
 
-        def quantise_w():
+        def copy_w():
             nc.scalar.copy(
                 out=w_grouped[:].rearrange("p (c i) t -> p c t i", i=4), in_=w_rows[:].rearrange("p t (c i) -> p c t i", i=4)
             )
+
+        def quantise_w():
             nc.vector.quantize_mx(
                 out=w_codes[:].bitcast(FP8X4), scales=w_scales[:], in_=w_grouped[:].rearrange("p n t -> p (n t)")
             )
@@ -120,179 +116,287 @@ def tile_selfattention_pa_kernel(tc, x_bytes, x_scale, freqs, w, b, g, out):
                 out=b_times_g[:], in0=b_and_g[:, 0:HEADS], in1=b_and_g[:, HEADS : 2 * HEADS], op=ALU.mult
             )
 
+        x_bf = []
+        x_grouped = []
         x_codes = []
         x_scales = []
-        gained = {}
-        inv_rms = {}
         msin_cos = []
+        for gi in range(GROUPS):
+            x_bf_g = per_group.tile([P, TILES * D], BF16, name="x_bf", tag="x_bf", align_bytes=64)
+            x_grouped_g = per_group.tile([P, TILES * D], BF16, name="x_grouped", tag="x_grouped", align_bytes=64)
+            codes_g = per_group.tile([P, D], U32, name="x_codes", tag="x_codes", align_bytes=64)
+            scales_g = per_group.tile([P, D], U8, name="x_scales", tag="x_scales", align_bytes=64)
+            msin_cos_g = per_group.tile([P, TILES * P], BF16, name="msin_cos", tag="msin_cos")
+            x_bf.append(x_bf_g)
+            x_grouped.append(x_grouped_g)
+            x_codes.append(codes_g)
+            x_scales.append(scales_g)
+            msin_cos.append(msin_cos_g)
 
-        def stage_a(gi):
-            x_bf = per_group.tile([P, TILES * D], BF16, name="x_bf", tag="x_bf", align_bytes=64)
-            x_grouped = per_group.tile([P, TILES * D], BF16, name="x_grouped", tag="x_grouped", align_bytes=64)
-            grouped_words = x_grouped[:].bitcast(F32)
-            for half in range(2):
-                turned = psum_turn.tile([P, D], F32, name="turned", tag="turn")
-                if gi >= WIDE_FROM:
-                    both = slice(half * 2 * D, (half + 1) * 2 * D)
-                    nc.vector.tensor_tensor(
-                        out=x_bf[:, both],
-                        in0=x_bytes_sb[:, gi, both].bitcast(FP8),
-                        in1=scale_all[:].rearrange("p c k -> p (c k)"),
-                        op=ALU.mult,
-                    )
-                for q2 in range(2):
-                    q = half * 2 + q2
+        def cast(gi, half):
+            both = slice(half * 2 * D, (half + 1) * 2 * D)
+            if gi == 0:
+                for q in (2 * half, 2 * half + 1):
                     cols = slice(q * D, (q + 1) * D)
-                    if gi < WIDE_FROM:
-                        nc.vector.tensor_tensor(
-                            out=x_bf[:, cols], in0=x_bytes_sb[:, gi, cols].bitcast(FP8), in1=scale_all[:, 0, :], op=ALU.mult
-                        )
-                    words = x_bf[:, cols].bitcast(F32)
-                    for u in range(2):
-                        c0 = (q2 * 2 + u) * P
-                        nc.tensor.transpose(
-                            out=turned[:, c0 : c0 + P], in_=words[:, u : D // 2 : 2], identity=token_perm[:]
-                        )
-                nc.scalar.copy(
-                    out=grouped_words[:, half * D : (half + 1) * D].rearrange("p (q n u) -> p q n u", q=2, u=2),
-                    in_=turned[:].rearrange("p (q u n) -> p q n u", q=2, u=2),
-                )
-            codes = per_group.tile([P, D], U32, name="x_codes", tag="x_codes", align_bytes=64)
-            scales = per_group.tile([P, D], U8, name="x_scales", tag="x_scales", align_bytes=64)
-            nc.vector.quantize_mx(out=codes[:].bitcast(FP8X4), scales=scales[:], in_=x_grouped[:])
-            x_codes.append(codes)
-            x_scales.append(scales)
+                    if half == 0:
+                        nc.vector.tensor_copy(out=x_bf[gi][:, cols], in_=x_bytes_sb[:, gi, cols].bitcast(FP8))
+                    else:
+                        nc.scalar.copy(out=x_bf[gi][:, cols], in_=x_bytes_sb[:, gi, cols].bitcast(FP8))
+            else:
+                nc.gpsimd.tensor_copy(out=x_bf[gi][:, both], in_=x_bytes_sb[:, gi, both].bitcast(FP8))
+
+        def turn_and_scale(gi, half):
+            both = slice(half * 2 * D, (half + 1) * 2 * D)
+            turned = psum_turn.tile([P, D], F32, name="turned", tag="turn")
+            for q2 in range(2):
+                q = half * 2 + q2
+                words = x_bf[gi][:, q * D : (q + 1) * D].bitcast(F32)
+                for u in range(2):
+                    c0 = (u * 2 + q2) * P
+                    nc.tensor.transpose(out=turned[:, c0 : c0 + P], in_=words[:, u : D // 2 : 2], identity=token_perm[:])
+            nc.vector.tensor_tensor(
+                out=x_grouped[gi][:, both].rearrange("p (c u e) -> p c u e", u=2, e=2),
+                in0=turned[:].bitcast(BF16).rearrange("p (u c e) -> p c u e", u=2, e=2),
+                in1=scale_cols[:].rearrange("p (o u e) -> p o u e", o=1, u=2).to_broadcast([P, 2 * P, 2, 2]),
+                op=ALU.mult,
+            )
+
+        def quantise_x(gi):
+            nc.vector.quantize_mx(out=x_codes[gi][:].bitcast(FP8X4), scales=x_scales[gi][:], in_=x_grouped[gi][:])
 
         def second_table(gi):
-            msin_cos_g = per_group.tile([P, TILES * P], BF16, name="msin_cos", tag="msin_cos")
             from_t = cos_sin[gi][:].rearrange("p (c f) -> p c f", f=2)
-            to_t = msin_cos_g[:].rearrange("p (c f) -> p c f", f=2)
+            to_t = msin_cos[gi][:].rearrange("p (c f) -> p c f", f=2)
             for f, factor in ((0, -1.0), (1, 1.0)):
                 nc.gpsimd.tensor_scalar(
                     out=to_t[:, :, f], in0=from_t[:, :, 1 - f], scalar1=factor, scalar2=0.0, op0=ALU.mult, op1=ALU.add
                 )
-            msin_cos.append(msin_cos_g)
 
-        def stage_b(unit):
-            gi, first, count = unit
-            tokens = slice(first * P, (first + count) * P)
-            width = count * P
-            gained_u = []
-            squares = []
-            def fill(h0):
-                acc_pair = psum_acc.tile([P, 2, D], F32, name="acc_pair", tag="acc")
-                for i in range(2):
-                    head = slice((h0 + i) * P, (h0 + i + 1) * P)
-                    nc.tensor.matmul_mx(
-                        out=acc_pair[:, i, 0:width],
-                        lhsT=w_codes[:, head].bitcast(FP8X4),
-                        lhsT_scale=w_scales[:, head],
-                        rhs=x_codes[gi][:, tokens].bitcast(FP8X4),
-                        rhs_scale=x_scales[gi][:, tokens],
-                        start=True,
-                        stop=True,
-                    )
-                return [acc_pair[:, 0, 0:width], acc_pair[:, 1, 0:width]]
+        squares = {}
+        gained = {}
+        inv_rms = {}
 
-            def square_of(h, acc):
-                square = per_head.tile([P, width], F32, name="square", tag="square")
-                nc.scalar.activation(out=square[:], in_=acc, func=ACT.Square, bias=b_and_g[:, h : h + 1], scale=1.0)
-                squares.append(square)
+        accs = {}
 
-            def gain_of(h, acc):
-                gained_h = per_head.tile([P, width], F32, name="gained", tag="gained")
-                nc.scalar.activation(
-                    out=gained_h[:],
-                    in_=acc,
-                    func=ACT.Identity,
-                    bias=b_times_g[:, h : h + 1],
-                    scale=b_and_g[:, HEADS + h : HEADS + h + 1],
+        def project(gi, h0):
+            acc_pair = psum_acc.tile([P, 2, D], F32, name="acc_pair", tag="acc")
+            for i in range(2):
+                head = slice((h0 + i) * P, (h0 + i + 1) * P)
+                nc.tensor.matmul_mx(
+                    out=acc_pair[:, i, :],
+                    lhsT=w_codes[:, head].bitcast(FP8X4),
+                    lhsT_scale=w_scales[:, head],
+                    rhs=x_codes[gi][:].bitcast(FP8X4),
+                    rhs_scale=x_scales[gi][:],
+                    start=True,
+                    stop=True,
                 )
-                gained_u.append(gained_h)
+                accs[gi, h0 + i] = acc_pair[:, i, :]
 
-            if unit == UNITS[-1]:
-                accs = fill(0) + fill(2)
-                for h in range(HEADS):
-                    square_of(h, accs[h])
-                for h in range(HEADS):
-                    gain_of(h, accs[h])
-            else:
-                for h0 in range(0, HEADS, 2):
-                    accs = fill(h0)
-                    for i in range(2):
-                        square_of(h0 + i, accs[i])
-                        gain_of(h0 + i, accs[i])
-            gained[unit] = gained_u
-            square_sums = psum_sq.tile([P, width], F32, name="square_sums", tag="square_sums")
-            for i in range(count):
+        def square(gi, h):
+            square_h = per_head.tile([P, D], F32, name="square", tag="square")
+            nc.scalar.activation(out=square_h[:], in_=accs[gi, h], func=ACT.Square, bias=b_and_g[:, h : h + 1], scale=1.0)
+            squares[gi, h] = square_h
+
+        def gain(gi, h):
+            gained_h = per_head.tile([P, D], F32, name="gained", tag="gained")
+            nc.scalar.activation(
+                out=gained_h[:],
+                in_=accs[gi, h],
+                func=ACT.Identity,
+                bias=b_times_g[:, h : h + 1],
+                scale=b_and_g[:, HEADS + h : HEADS + h + 1],
+            )
+            gained[gi, h] = gained_h
+
+        square_sums = {}
+
+        def turn_squares(gi, half):
+            if half == 0:
+                square_sums_g = psum_sq.tile([P, D], F32, name="square_sums", tag="square_sums")
+                square_sums[gi] = square_sums_g
+            square_sums_g = square_sums[gi]
+            for i in (2 * half, 2 * half + 1):
                 for h in range(HEADS):
                     nc.tensor.matmul(
-                        out=square_sums[:, i * P : (i + 1) * P],
-                        lhsT=squares[h][:, i * P : (i + 1) * P],
+                        out=square_sums_g[:, i * P : (i + 1) * P],
+                        lhsT=squares[gi, h][:, i * P : (i + 1) * P],
                         rhs=identity[:],
                         is_transpose=True,
                         start=(h == 0),
                         stop=(h == HEADS - 1),
                     )
-            total = per_unit.tile([P, count], F32, name="total", tag="total")
-            for i in range(count):
+
+        def rms(gi):
+            total = per_group.tile([P, TILES], F32, name="total", tag="total")
+            for i in range(TILES):
                 unused = per_tile.tile([P, P], F32, name="unused", tag="unused")
                 nc.scalar.activation(
-                    out=unused[:], in_=square_sums[:, i * P : (i + 1) * P], func=ACT.Copy, accum_out=total[:, i : i + 1]
+                    out=unused[:], in_=square_sums[gi][:, i * P : (i + 1) * P], func=ACT.Copy, accum_out=total[:, i : i + 1]
                 )
-            inv_rms_u = per_unit.tile([P, count], F32, name="inv_rms", tag="inv_rms")
-            nc.scalar.activation(out=inv_rms_u[:], in_=total[:], func=ACT.Abs_reciprocal_sqrt, bias=EPS, scale=1.0 / D)
-            inv_rms[unit] = inv_rms_u
+            inv_rms_g = per_group.tile([P, TILES], F32, name="inv_rms", tag="inv_rms")
+            nc.scalar.activation(out=inv_rms_g[:], in_=total[:], func=ACT.Abs_reciprocal_sqrt, bias=EPS, scale=1.0 / D)
+            inv_rms[gi] = inv_rms_g
 
-        def stage_c(unit):
-            gi, first, count = unit
-            by_pair = [P, HEADS, PAIRS, 2]
-            for start in range(0, count, 2):
+        by_pair = [P, HEADS, PAIRS, 2]
+
+        rope_tiles = {}
+
+        def rope(tile):
+            gi, q = tile // TILES, tile % TILES
+            i = tile % 2
+            if i == 0:
                 products = []
                 for e in range(2):
                     product = per_tile.tile([P, 2, D], F32, name="product%d" % e, tag="product%d" % e)
                     products.append(product)
-                rotated = per_tile.tile([P, 2, D], F32, name="rotated", tag="rotated")
+                rope_tiles[tile // 2] = products
+            products = rope_tiles[tile // 2]
+            y_tokens = psum_turn.tile([P, D], F32, name="y_tokens", tag="turn")
+            for h in range(HEADS):
+                nc.tensor.transpose(
+                    out=y_tokens[:, h * P : (h + 1) * P],
+                    in_=gained[gi, h][:, q * P : (q + 1) * P],
+                    identity=identity[:],
+                )
+            pairs = y_tokens[:].rearrange("p (h j e) -> p h j e", h=HEADS, e=2)
+            for e, table in ((0, cos_sin[gi]), (1, msin_cos[gi])):
+                nc.vector.scalar_tensor_tensor(
+                    out=products[e][:, i, :].rearrange("p (h j f) -> p h j f", h=HEADS, f=2),
+                    in0=pairs[:, :, :, e : e + 1].to_broadcast(by_pair),
+                    scalar=inv_rms[gi][:, q : q + 1],
+                    in1=table[:, q * P : (q + 1) * P].rearrange("p (o j f) -> p o j f", o=1, f=2).to_broadcast(by_pair),
+                    op0=ALU.mult,
+                    op1=ALU.mult,
+                )
+            if i == 0:
+                return
+            rotated = per_tile.tile([P, 2, D], F32, name="rotated", tag="rotated")
+            if tile == TILES * GROUPS - 1:
                 for i in range(2):
-                    q = first + start + i
-                    y_tokens = psum_turn.tile([P, D], F32, name="y_tokens", tag="turn")
-                    for h in range(HEADS):
-                        nc.tensor.transpose(
-                            out=y_tokens[:, h * P : (h + 1) * P],
-                            in_=gained[unit][h][:, (start + i) * P : (start + i + 1) * P],
-                            identity=identity[:],
-                        )
-                    pairs = y_tokens[:].rearrange("p (h j e) -> p h j e", h=HEADS, e=2)
-                    for e, table in ((0, cos_sin[gi]), (1, msin_cos[gi])):
-                        nc.vector.scalar_tensor_tensor(
-                            out=products[e][:, i, :].rearrange("p (h j f) -> p h j f", h=HEADS, f=2),
-                            in0=pairs[:, :, :, e : e + 1].to_broadcast(by_pair),
-                            scalar=inv_rms[unit][:, start + i : start + i + 1],
-                            in1=table[:, q * P : (q + 1) * P].rearrange("p (o j f) -> p o j f", o=1, f=2).to_broadcast(by_pair),
-                            op0=ALU.mult,
-                            op1=ALU.mult,
-                        )
-                if unit == UNITS[-1]:
-                    for i in range(2):
-                        nc.vector.tensor_tensor(
-                            out=rotated[:, i, :], in0=products[0][:, i, :], in1=products[1][:, i, :], op=ALU.add
-                        )
-                else:
-                    nc.gpsimd.tensor_tensor(out=rotated[:], in0=products[0][:], in1=products[1][:], op=ALU.add)
-                for i in range(2):
-                    nc.sync.dma_start(out=out_by_tile[gi, first + start + i], in_=rotated[:, i, :])
+                    nc.vector.tensor_tensor(
+                        out=rotated[:, i, :], in0=products[0][:, i, :], in1=products[1][:, i, :], op=ALU.add
+                    )
+            else:
+                nc.gpsimd.tensor_tensor(out=rotated[:], in0=products[0][:], in1=products[1][:], op=ALU.add)
+            for i in range(2):
+                nc.sync.dma_start(out=out_by_tile[gi, q - 1 + i], in_=rotated[:, i, :])
 
-        for gi in range(A_LEAD):
-            stage_a(gi)
-            if gi == 0:
-                quantise_w()
-                bias_and_gain_to_partitions()
-        for gi in range(GROUPS):
-            second_table(gi)
-        for step in range(len(UNITS) + C_LAG):
-            if step >= C_LAG:
-                stage_c(UNITS[step - C_LAG])
-            if step < len(UNITS):
-                stage_b(UNITS[step])
-            if step + A_LEAD < GROUPS:
-                stage_a(step + A_LEAD)
+        cast(0, 0)
+        cast(0, 1)
+        copy_w()
+        turn_and_scale(0, 0)
+        turn_and_scale(0, 1)
+        bias_and_gain_to_partitions()
+        quantise_w()
+        quantise_x(0)
+        cast(1, 0)
+        cast(1, 1)
+        cast(2, 0)
+        cast(2, 1)
+        cast(3, 0)
+        cast(3, 1)
+        second_table(0)
+        cast(4, 0)
+        cast(4, 1)
+        second_table(1)
+        second_table(2)
+        second_table(3)
+        second_table(4)
+        turn_and_scale(1, 0)
+        turn_and_scale(1, 1)
+        quantise_x(1)
+        project(0, 0)
+        project(0, 2)
+        square(0, 0)
+        square(0, 1)
+        gain(0, 0)
+        gain(0, 1)
+        square(0, 2)
+        square(0, 3)
+        gain(0, 2)
+        gain(0, 3)
+        turn_and_scale(2, 0)
+        turn_and_scale(2, 1)
+        quantise_x(2)
+        turn_and_scale(3, 0)
+        project(1, 0)
+        square(1, 0)
+        turn_squares(0, 0)
+        turn_squares(0, 1)
+        rms(0)
+        square(1, 1)
+        gain(1, 0)
+        gain(1, 1)
+        rope(0)
+        project(1, 2)
+        square(1, 2)
+        square(1, 3)
+        gain(1, 2)
+        gain(1, 3)
+        rope(1)
+        turn_and_scale(3, 1)
+        quantise_x(3)
+        project(2, 0)
+        square(2, 0)
+        rope(2)
+        turn_squares(1, 0)
+        turn_squares(1, 1)
+        rms(1)
+        square(2, 1)
+        gain(2, 0)
+        gain(2, 1)
+        rope(3)
+        project(2, 2)
+        square(2, 2)
+        square(2, 3)
+        gain(2, 2)
+        gain(2, 3)
+        turn_and_scale(4, 0)
+        turn_and_scale(4, 1)
+        quantise_x(4)
+        project(3, 0)
+        square(3, 0)
+        rope(4)
+        turn_squares(2, 0)
+        turn_squares(2, 1)
+        rms(2)
+        square(3, 1)
+        gain(3, 0)
+        gain(3, 1)
+        rope(5)
+        project(3, 2)
+        square(3, 2)
+        square(3, 3)
+        gain(3, 2)
+        gain(3, 3)
+        rope(6)
+        rope(7)
+        project(4, 0)
+        square(4, 0)
+        rope(8)
+        turn_squares(3, 0)
+        turn_squares(3, 1)
+        rms(3)
+        square(4, 1)
+        gain(4, 0)
+        gain(4, 1)
+        rope(9)
+        rope(10)
+        project(4, 2)
+        square(4, 2)
+        square(4, 3)
+        gain(4, 2)
+        gain(4, 3)
+        rope(11)
+        rope(12)
+        rope(13)
+        turn_squares(4, 0)
+        turn_squares(4, 1)
+        rms(4)
+        rope(14)
+        rope(15)
+        rope(16)
+        rope(17)
+        rope(18)
+        rope(19)

@@ -135,15 +135,14 @@ def tile_selfattention_pa_kernel(tc, x_bytes, x_scale, freqs, w, b, g, out):
 
         def cast(gi, half):
             both = slice(half * 2 * D, (half + 1) * 2 * D)
-            if gi == 0:
-                for q in (2 * half, 2 * half + 1):
-                    cols = slice(q * D, (q + 1) * D)
-                    if half == 0:
-                        nc.vector.tensor_copy(out=x_bf[gi][:, cols], in_=x_bytes_sb[:, gi, cols].bitcast(FP8))
-                    else:
-                        nc.scalar.copy(out=x_bf[gi][:, cols], in_=x_bytes_sb[:, gi, cols].bitcast(FP8))
-            else:
-                nc.gpsimd.tensor_copy(out=x_bf[gi][:, both], in_=x_bytes_sb[:, gi, both].bitcast(FP8))
+            for q in (2 * half, 2 * half + 1):
+                cols = slice(q * D, (q + 1) * D)
+                if gi == 0 and half == 0:
+                    nc.vector.tensor_copy(out=x_bf[gi][:, cols], in_=x_bytes_sb[:, gi, cols].bitcast(FP8))
+                elif gi < 2:
+                    nc.scalar.copy(out=x_bf[gi][:, cols], in_=x_bytes_sb[:, gi, cols].bitcast(FP8))
+                else:
+                    nc.gpsimd.tensor_copy(out=x_bf[gi][:, cols], in_=x_bytes_sb[:, gi, cols].bitcast(FP8))
 
         def turn_and_scale(gi, half):
             both = slice(half * 2 * D, (half + 1) * 2 * D)
@@ -336,10 +335,10 @@ def tile_selfattention_pa_kernel(tc, x_bytes, x_scale, freqs, w, b, g, out):
         gain(1, 3)
         rope(1)
         turn_and_scale(3, 1)
-        quantise_x(3)
         project(2, 0)
         square(2, 0)
         rope(2)
+        quantise_x(3)
         turn_squares(1, 0)
         turn_squares(1, 1)
         rms(1)
@@ -347,54 +346,54 @@ def tile_selfattention_pa_kernel(tc, x_bytes, x_scale, freqs, w, b, g, out):
         gain(2, 0)
         gain(2, 1)
         rope(3)
+        turn_and_scale(4, 0)
+        turn_and_scale(4, 1)
         project(2, 2)
         square(2, 2)
         square(2, 3)
         gain(2, 2)
         gain(2, 3)
-        turn_and_scale(4, 0)
-        turn_and_scale(4, 1)
+        rope(4)
         quantise_x(4)
         project(3, 0)
         square(3, 0)
-        rope(4)
+        rope(5)
         turn_squares(2, 0)
         turn_squares(2, 1)
         rms(2)
         square(3, 1)
         gain(3, 0)
         gain(3, 1)
-        rope(5)
+        rope(6)
         project(3, 2)
         square(3, 2)
         square(3, 3)
         gain(3, 2)
         gain(3, 3)
-        rope(6)
         rope(7)
+        rope(8)
         project(4, 0)
         square(4, 0)
-        rope(8)
+        rope(9)
         turn_squares(3, 0)
         turn_squares(3, 1)
         rms(3)
         square(4, 1)
         gain(4, 0)
         gain(4, 1)
-        rope(9)
         rope(10)
+        rope(11)
         project(4, 2)
         square(4, 2)
         square(4, 3)
         gain(4, 2)
         gain(4, 3)
-        rope(11)
         rope(12)
         rope(13)
+        rope(14)
         turn_squares(4, 0)
         turn_squares(4, 1)
         rms(4)
-        rope(14)
         rope(15)
         rope(16)
         rope(17)

@@ -21,6 +21,7 @@ PACK = 4
 GROUPS = 5
 TILES = 4
 EPS = 1e-5
+LAST_TILES = 16
 FLOPS = 2 * TOKENS * D * D
 
 
@@ -55,7 +56,9 @@ def tile_selfattention_pa_kernel(tc, x_bytes, x_scale, freqs, w, b, g, out):
         def load_x(gi):
             nc.sync.dma_start(out=x_bytes_sb[:, gi, :], in_=x_by_group[gi])
 
-        load_x(0)
+        for half in range(2):
+            both = slice(half * 2 * D, (half + 1) * 2 * D)
+            nc.sync.dma_start(out=x_bytes_sb[:, 0, both], in_=x_by_group[0][:, both])
         nc.sync.dma_start(out=scale_cols[:], in_=x_scale.rearrange("a b (p t) -> (a b p) t", t=PACK))
         nc.sync.dma_start(out=w_rows[:], in_=w.rearrange("(p t) n -> p t n", t=PACK))
         load_x(1)
@@ -139,7 +142,7 @@ def tile_selfattention_pa_kernel(tc, x_bytes, x_scale, freqs, w, b, g, out):
                 cols = slice(q * D, (q + 1) * D)
                 if gi == 0 and half == 0:
                     nc.vector.tensor_copy(out=x_bf[gi][:, cols], in_=x_bytes_sb[:, gi, cols].bitcast(FP8))
-                elif gi < 2:
+                elif gi == 0 or (gi == 1 and half == 1):
                     nc.scalar.copy(out=x_bf[gi][:, cols], in_=x_bytes_sb[:, gi, cols].bitcast(FP8))
                 else:
                     nc.gpsimd.tensor_copy(out=x_bf[gi][:, cols], in_=x_bytes_sb[:, gi, cols].bitcast(FP8))
@@ -269,17 +272,20 @@ def tile_selfattention_pa_kernel(tc, x_bytes, x_scale, freqs, w, b, g, out):
                     op1=ALU.mult,
                 )
             if i == 0:
-                return
-            rotated = per_tile.tile([P, 2, D], F32, name="rotated", tag="rotated")
-            if tile == TILES * GROUPS - 1:
-                for i in range(2):
-                    nc.vector.tensor_tensor(
-                        out=rotated[:, i, :], in0=products[0][:, i, :], in1=products[1][:, i, :], op=ALU.add
-                    )
-            else:
-                nc.gpsimd.tensor_tensor(out=rotated[:], in0=products[0][:], in1=products[1][:], op=ALU.add)
-            for i in range(2):
-                nc.sync.dma_start(out=out_by_tile[gi, q - 1 + i], in_=rotated[:, i, :])
+                rotated = per_tile.tile([P, 2, D], F32, name="rotated", tag="rotated")
+                products.append(rotated)
+            if tile < LAST_TILES:
+                if i == 1:
+                    rotated = products[2]
+                    nc.gpsimd.tensor_tensor(out=rotated[:], in0=products[0][:], in1=products[1][:], op=ALU.add)
+                    for i in range(2):
+                        nc.sync.dma_start(out=out_by_tile[gi, q - 1 + i], in_=rotated[:, i, :])
+
+        def add(tile, engine):
+            p0, p1, rotated = rope_tiles[tile // 2]
+            i = tile % 2
+            engine.tensor_tensor(out=rotated[:, i, :], in0=p0[:, i, :], in1=p1[:, i, :], op=ALU.add)
+            nc.sync.dma_start(out=out_by_tile[tile // TILES, tile % TILES], in_=rotated[:, i, :])
 
         cast(0, 0)
         cast(0, 1)
@@ -321,10 +327,10 @@ def tile_selfattention_pa_kernel(tc, x_bytes, x_scale, freqs, w, b, g, out):
         turn_and_scale(3, 0)
         project(1, 0)
         square(1, 0)
+        square(1, 1)
         turn_squares(0, 0)
         turn_squares(0, 1)
         rms(0)
-        square(1, 1)
         gain(1, 0)
         gain(1, 1)
         rope(0)
@@ -337,12 +343,12 @@ def tile_selfattention_pa_kernel(tc, x_bytes, x_scale, freqs, w, b, g, out):
         turn_and_scale(3, 1)
         project(2, 0)
         square(2, 0)
+        square(2, 1)
         rope(2)
         quantise_x(3)
         turn_squares(1, 0)
         turn_squares(1, 1)
         rms(1)
-        square(2, 1)
         gain(2, 0)
         gain(2, 1)
         rope(3)
@@ -357,11 +363,11 @@ def tile_selfattention_pa_kernel(tc, x_bytes, x_scale, freqs, w, b, g, out):
         quantise_x(4)
         project(3, 0)
         square(3, 0)
+        square(3, 1)
         rope(5)
         turn_squares(2, 0)
         turn_squares(2, 1)
         rms(2)
-        square(3, 1)
         gain(3, 0)
         gain(3, 1)
         rope(6)
@@ -374,11 +380,11 @@ def tile_selfattention_pa_kernel(tc, x_bytes, x_scale, freqs, w, b, g, out):
         rope(8)
         project(4, 0)
         square(4, 0)
+        square(4, 1)
         rope(9)
         turn_squares(3, 0)
         turn_squares(3, 1)
         rms(3)
-        square(4, 1)
         gain(4, 0)
         gain(4, 1)
         rope(10)
@@ -397,5 +403,9 @@ def tile_selfattention_pa_kernel(tc, x_bytes, x_scale, freqs, w, b, g, out):
         rope(15)
         rope(16)
         rope(17)
+        add(16, nc.gpsimd)
         rope(18)
         rope(19)
+        add(17, nc.vector)
+        add(18, nc.vector)
+        add(19, nc.vector)

@@ -142,7 +142,7 @@ def tile_selfattention_pa_kernel(tc, x_bytes, x_scale, freqs, w, b, g, out):
                 cols = slice(q * D, (q + 1) * D)
                 if gi == 0 and half == 0:
                     nc.vector.tensor_copy(out=x_bf[gi][:, cols], in_=x_bytes_sb[:, gi, cols].bitcast(FP8))
-                elif gi == 0 or (gi == 1 and half == 1):
+                elif gi < 2:
                     nc.scalar.copy(out=x_bf[gi][:, cols], in_=x_bytes_sb[:, gi, cols].bitcast(FP8))
                 else:
                     nc.gpsimd.tensor_copy(out=x_bf[gi][:, cols], in_=x_bytes_sb[:, gi, cols].bitcast(FP8))
@@ -292,9 +292,9 @@ def tile_selfattention_pa_kernel(tc, x_bytes, x_scale, freqs, w, b, g, out):
         copy_w()
         turn_and_scale(0, 0)
         turn_and_scale(0, 1)
-        bias_and_gain_to_partitions()
         quantise_w()
         quantise_x(0)
+        bias_and_gain_to_partitions()
         cast(1, 0)
         cast(1, 1)
         cast(2, 0)
@@ -333,6 +333,7 @@ def tile_selfattention_pa_kernel(tc, x_bytes, x_scale, freqs, w, b, g, out):
         rms(0)
         gain(1, 0)
         gain(1, 1)
+        turn_and_scale(3, 1)
         rope(0)
         project(1, 2)
         square(1, 2)
@@ -340,31 +341,30 @@ def tile_selfattention_pa_kernel(tc, x_bytes, x_scale, freqs, w, b, g, out):
         gain(1, 2)
         gain(1, 3)
         rope(1)
-        turn_and_scale(3, 1)
+        quantise_x(3)
         project(2, 0)
         square(2, 0)
         square(2, 1)
         rope(2)
-        quantise_x(3)
         turn_squares(1, 0)
         turn_squares(1, 1)
         rms(1)
         gain(2, 0)
         gain(2, 1)
         rope(3)
-        turn_and_scale(4, 0)
-        turn_and_scale(4, 1)
         project(2, 2)
         square(2, 2)
         square(2, 3)
         gain(2, 2)
         gain(2, 3)
         rope(4)
-        quantise_x(4)
+        turn_and_scale(4, 0)
+        turn_and_scale(4, 1)
         project(3, 0)
         square(3, 0)
         square(3, 1)
         rope(5)
+        quantise_x(4)
         turn_squares(2, 0)
         turn_squares(2, 1)
         rms(2)
@@ -378,29 +378,29 @@ def tile_selfattention_pa_kernel(tc, x_bytes, x_scale, freqs, w, b, g, out):
         gain(3, 3)
         rope(7)
         rope(8)
+        rope(9)
         project(4, 0)
         square(4, 0)
         square(4, 1)
-        rope(9)
+        rope(10)
         turn_squares(3, 0)
         turn_squares(3, 1)
         rms(3)
         gain(4, 0)
         gain(4, 1)
-        rope(10)
         rope(11)
+        rope(12)
         project(4, 2)
         square(4, 2)
         square(4, 3)
         gain(4, 2)
         gain(4, 3)
-        rope(12)
         rope(13)
         rope(14)
+        rope(15)
         turn_squares(4, 0)
         turn_squares(4, 1)
         rms(4)
-        rope(15)
         rope(16)
         rope(17)
         add(16, nc.gpsimd)

@@ -116,7 +116,7 @@ def tile_selfattention_pa_kernel(tc, x_bytes, x_scale, freqs, w, b, g, out):
             nc.tensor.transpose(out=turned[:], in_=bg_rows[:], identity=identity_bf[:])
             nc.vector.tensor_copy(out=b_and_g[:], in_=turned[:, 0 : 2 * HEADS])
             nc.vector.tensor_tensor(
-                out=b_times_g[:], in0=b_and_g[:, 0:HEADS], in1=b_and_g[:, HEADS : 2 * HEADS], op=ALU.mult
+                out=b_times_g[:], in0=turned[:, 0:HEADS], in1=b_and_g[:, HEADS : 2 * HEADS], op=ALU.mult
             )
 
         x_bf = []
@@ -142,7 +142,7 @@ def tile_selfattention_pa_kernel(tc, x_bytes, x_scale, freqs, w, b, g, out):
                 cols = slice(q * D, (q + 1) * D)
                 if gi == 0 and half == 0:
                     nc.vector.tensor_copy(out=x_bf[gi][:, cols], in_=x_bytes_sb[:, gi, cols].bitcast(FP8))
-                elif gi < 2:
+                elif gi == 0 or (gi == 1 and half == 1):
                     nc.scalar.copy(out=x_bf[gi][:, cols], in_=x_bytes_sb[:, gi, cols].bitcast(FP8))
                 else:
                     nc.gpsimd.tensor_copy(out=x_bf[gi][:, cols], in_=x_bytes_sb[:, gi, cols].bitcast(FP8))

@@ -123,18 +123,18 @@ def tile_selfattention_pa_kernel(tc, x_bytes, x_scale, freqs, w, b, g, out):
         x_grouped = []
         x_codes = []
         x_scales = []
-        msin_cos = []
+        cos_msin = []
         for gi in range(GROUPS):
             x_bf_g = per_group.tile([P, TILES * D], BF16, name="x_bf", tag="x_bf", align_bytes=64)
             x_grouped_g = per_group.tile([P, TILES * D], BF16, name="x_grouped", tag="x_grouped", align_bytes=64)
             codes_g = per_group.tile([P, D], U32, name="x_codes", tag="x_codes", align_bytes=64)
             scales_g = per_group.tile([P, D], U8, name="x_scales", tag="x_scales", align_bytes=64)
-            msin_cos_g = per_group.tile([P, TILES * P], BF16, name="msin_cos", tag="msin_cos")
+            cos_msin_g = per_group.tile([P, TILES * P], BF16, name="cos_msin", tag="cos_msin")
             x_bf.append(x_bf_g)
             x_grouped.append(x_grouped_g)
             x_codes.append(codes_g)
             x_scales.append(scales_g)
-            msin_cos.append(msin_cos_g)
+            cos_msin.append(cos_msin_g)
 
         def cast(gi, half):
             both = slice(half * 2 * D, (half + 1) * 2 * D)
@@ -167,12 +167,13 @@ def tile_selfattention_pa_kernel(tc, x_bytes, x_scale, freqs, w, b, g, out):
             nc.vector.quantize_mx(out=x_codes[gi][:].bitcast(FP8X4), scales=x_scales[gi][:], in_=x_grouped[gi][:])
 
         def second_table(gi):
-            from_t = cos_sin[gi][:].rearrange("p (c f) -> p c f", f=2)
-            to_t = msin_cos[gi][:].rearrange("p (c f) -> p c f", f=2)
-            for f, factor in ((0, -1.0), (1, 1.0)):
-                nc.gpsimd.tensor_scalar(
-                    out=to_t[:, :, f], in0=from_t[:, :, 1 - f], scalar1=factor, scalar2=0.0, op0=ALU.mult, op1=ALU.add
-                )
+            nc.vector.tensor_scalar(
+                out=cos_msin[gi][:].bitcast(I32),
+                in0=cos_sin[gi][:].bitcast(I32),
+                scalar1=-0x80000000,
+                scalar2=None,
+                op0=ALU.bitwise_xor,
+            )
 
         squares = {}
         gained = {}
@@ -262,9 +263,9 @@ def tile_selfattention_pa_kernel(tc, x_bytes, x_scale, freqs, w, b, g, out):
                     identity=identity[:],
                 )
             pairs = y_tokens[:].rearrange("p (h j e) -> p h j e", h=HEADS, e=2)
-            for e, table in ((0, cos_sin[gi]), (1, msin_cos[gi])):
+            for e, table, step in ((0, cos_sin[gi], 1), (1, cos_msin[gi], -1)):
                 nc.vector.scalar_tensor_tensor(
-                    out=products[e][:, i, :].rearrange("p (h j f) -> p h j f", h=HEADS, f=2),
+                    out=products[e][:, i, :].rearrange("p (h j f) -> p h j f", h=HEADS, f=2)[:, :, :, ::step],
                     in0=pairs[:, :, :, e : e + 1].to_broadcast(by_pair),
                     scalar=inv_rms[gi][:, q : q + 1],
                     in1=table[:, q * P : (q + 1) * P].rearrange("p (o j f) -> p o j f", o=1, f=2).to_broadcast(by_pair),
@@ -301,13 +302,8 @@ def tile_selfattention_pa_kernel(tc, x_bytes, x_scale, freqs, w, b, g, out):
         cast(2, 1)
         cast(3, 0)
         cast(3, 1)
-        second_table(0)
         cast(4, 0)
         cast(4, 1)
-        second_table(1)
-        second_table(2)
-        second_table(3)
-        second_table(4)
         turn_and_scale(1, 0)
         turn_and_scale(1, 1)
         quantise_x(1)
@@ -325,6 +321,11 @@ def tile_selfattention_pa_kernel(tc, x_bytes, x_scale, freqs, w, b, g, out):
         turn_and_scale(2, 1)
         quantise_x(2)
         turn_and_scale(3, 0)
+        second_table(0)
+        second_table(1)
+        second_table(2)
+        second_table(3)
+        second_table(4)
         project(1, 0)
         square(1, 0)
         square(1, 1)
@@ -386,20 +387,20 @@ def tile_selfattention_pa_kernel(tc, x_bytes, x_scale, freqs, w, b, g, out):
         turn_squares(3, 0)
         turn_squares(3, 1)
         rms(3)
-        gain(4, 0)
-        gain(4, 1)
         rope(11)
         rope(12)
         project(4, 2)
         square(4, 2)
         square(4, 3)
+        gain(4, 0)
+        gain(4, 1)
         gain(4, 2)
         gain(4, 3)
         rope(13)
         rope(14)
-        rope(15)
         turn_squares(4, 0)
         turn_squares(4, 1)
+        rope(15)
         rms(4)
         rope(16)
         rope(17)

from contextlib import ExitStack

import concourse.mybir as mybir

F32 = mybir.dt.float32
BF16 = mybir.dt.bfloat16
I32 = mybir.dt.int32
U32 = mybir.dt.uint32
U8 = mybir.dt.uint8
FP8 = mybir.dt.float8_e4m3fn
FP8X4 = mybir.dt.float8_e4m3fn_x4
ALU = mybir.AluOpType
ACT = mybir.ActivationFunctionType

P = 128
TOKENS = 2560
D = 512
HEADS = 4
PAIRS = 64
PACK = 4
GROUPS = 5
TILES = 4
EPS = 1e-5
LAST_TILES = 16
FLOPS = 2 * TOKENS * D * D


def tile_selfattention_pa_kernel(tc, x_bytes, x_scale, freqs, w, b, g, out):
    nc = tc.nc
    x_by_group = x_bytes.rearrange("o (g p q) k -> (o g) p (q k)", p=P, q=TILES)
    freqs_by_window = freqs.rearrange(
        "(g fi ho hi wo q) o j f -> g ho wo fi hi (q o j f)", g=GROUPS, fi=8, ho=2, hi=4, wo=2, q=TILES
    )
    out_by_tile = out.rearrange("o (g hw a q) f -> (o g) q a hw f", g=GROUPS, hw=4, a=32, q=TILES)

    with ExitStack() as ctx:
        const = ctx.enter_context(tc.tile_pool(name="const", bufs=1))
        per_group = ctx.enter_context(tc.tile_pool(name="per_group", bufs=GROUPS))
        per_head = ctx.enter_context(tc.tile_pool(name="per_head", bufs=3 * HEADS))
        per_tile = ctx.enter_context(tc.tile_pool(name="per_tile", bufs=4))
        psum_turn = ctx.enter_context(tc.psum_pool(name="psum_turn", bufs=3))
        psum_acc = ctx.enter_context(tc.psum_pool(name="psum_acc", bufs=2))
        psum_sq = ctx.enter_context(tc.psum_pool(name="psum_sq", bufs=1))
        ctx.enter_context(tc.manual_schedule())

        x_bytes_sb = const.tile([P, GROUPS, TILES * D], U8, name="x_bytes_sb")
        scale_cols = const.tile([P, PACK], F32, name="scale_cols")
        w_rows = const.tile([P, PACK, D], BF16, name="w_rows")
        bg_rows = const.tile([P, P], BF16, name="bg_rows")
        cos_sin = []
        for gi in range(GROUPS):
            cos_sin_g = per_group.tile([P, TILES * P], BF16, name="cos_sin", tag="cos_sin")
            cos_sin.append(cos_sin_g)
        nc.vector.memset(bg_rows[:], 0.0)

        def load_x(gi):
            nc.sync.dma_start(out=x_bytes_sb[:, gi, :], in_=x_by_group[gi])

        for half in range(2):
            both = slice(half * 2 * D, (half + 1) * 2 * D)
            nc.sync.dma_start(out=x_bytes_sb[:, 0, both], in_=x_by_group[0][:, both])
        nc.sync.dma_start(out=scale_cols[:], in_=x_scale.rearrange("a b (p t) -> (a b p) t", t=PACK))
        nc.sync.dma_start(out=w_rows[:], in_=w.rearrange("(p t) n -> p t n", t=PACK))
        load_x(1)
        nc.sync.dma_start(out=bg_rows[0:HEADS, :], in_=b.rearrange("(h p) -> h p", p=P))
        nc.sync.dma_start(out=bg_rows[HEADS : 2 * HEADS, :], in_=g.rearrange("(h p) -> h p", p=P))
        for gi in range(2, GROUPS):
            load_x(gi)
        for gi in range(GROUPS):
            for hw in range(4):
                nc.sync.dma_start(out=cos_sin[gi][hw : P : 4, :], in_=freqs_by_window[gi, hw // 2, hw % 2])

        ones = const.tile([P, 32], F32, name="ones", align_bytes=64)
        nc.vector.memset(ones[:], 1.0)
        table_warm = const.tile([P, 1], F32, name="table_warm")
        nc.scalar.activation(out=table_warm[:], in_=ones[:, 0:1], func=ACT.Abs_reciprocal_sqrt)
        column_no = const.tile([P, 32], F32, name="column_no", align_bytes=64)
        nc.vector.tensor_tensor_scan(
            out=column_no[:], data0=ones[:], data1=ones[:], initial=0.0, op0=ALU.mult, op1=ALU.add
        )
        partition_no = const.tile([P, 32], F32, name="partition_no", align_bytes=64)
        nc.vector.transpose(out=partition_no[:], in_=column_no[:])
        identity = const.tile([P, P], F32, name="identity")
        nc.vector.memset(identity[:], 0.0)
        for blk in range(4):
            rows = slice(blk * 32, (blk + 1) * 32)
            nc.vector.tensor_tensor(
                out=identity[rows, rows], in0=column_no[rows, :], in1=partition_no[rows, :], op=ALU.is_equal
            )
        token_perm = const.tile([P, P], F32, name="token_perm")
        from_v = identity[:].rearrange("p (fi ho hi wo) -> p ho fi hi wo", fi=8, ho=2, hi=4, wo=2)
        to_v = token_perm[:].rearrange("p (fi hi ho wo) -> p ho fi hi wo", fi=8, ho=2, hi=4, wo=2)
        for ho in range(2):
            nc.vector.tensor_copy(out=to_v[:, ho], in_=from_v[:, ho])
        identity_bf = const.tile([P, P], BF16, name="identity_bf")
        nc.vector.tensor_copy(out=identity_bf[:], in_=identity[:])

        b_and_g = const.tile([P, 2 * HEADS], F32, name="b_and_g")
        b_times_g = const.tile([P, HEADS], F32, name="b_times_g")
        w_grouped = const.tile([P, D, PACK], BF16, name="w_grouped", align_bytes=64)
        w_codes = const.tile([P, D], U32, name="w_codes", align_bytes=64)
        w_scales = const.tile([P, D], U8, name="w_scales", align_bytes=64)

        def copy_w():
            nc.scalar.copy(
                out=w_grouped[:].rearrange("p (c i) t -> p c t i", i=4), in_=w_rows[:].rearrange("p t (c i) -> p c t i", i=4)
            )

        def quantise_w():
            nc.vector.quantize_mx(
                out=w_codes[:].bitcast(FP8X4), scales=w_scales[:], in_=w_grouped[:].rearrange("p n t -> p (n t)")
            )

        def bias_and_gain_to_partitions():
            turned = psum_turn.tile([P, P], BF16, name="turned", tag="turn")
            nc.tensor.transpose(out=turned[:], in_=bg_rows[:], identity=identity_bf[:])
            nc.vector.tensor_copy(out=b_and_g[:], in_=turned[:, 0 : 2 * HEADS])
            nc.vector.tensor_tensor(
                out=b_times_g[:], in0=turned[:, 0:HEADS], in1=b_and_g[:, HEADS : 2 * HEADS], op=ALU.mult
            )

        x_bf = []
        x_grouped = []
        x_codes = []
        x_scales = []
        cos_msin = []
        for gi in range(GROUPS):
            x_bf_g = per_group.tile([P, TILES * D], BF16, name="x_bf", tag="x_bf", align_bytes=64)
            x_grouped_g = per_group.tile([P, TILES * D], BF16, name="x_grouped", tag="x_grouped", align_bytes=64)
            codes_g = per_group.tile([P, D], U32, name="x_codes", tag="x_codes", align_bytes=64)
            scales_g = per_group.tile([P, D], U8, name="x_scales", tag="x_scales", align_bytes=64)
            cos_msin_g = per_group.tile([P, TILES * P], BF16, name="cos_msin", tag="cos_msin")
            x_bf.append(x_bf_g)
            x_grouped.append(x_grouped_g)
            x_codes.append(codes_g)
            x_scales.append(scales_g)
            cos_msin.append(cos_msin_g)

        def cast(gi, half):
            both = slice(half * 2 * D, (half + 1) * 2 * D)
            for q in (2 * half, 2 * half + 1):
                cols = slice(q * D, (q + 1) * D)
                if gi == 0 and half == 0:
                    nc.vector.tensor_copy(out=x_bf[gi][:, cols], in_=x_bytes_sb[:, gi, cols].bitcast(FP8))
                elif gi == 0 or (gi == 1 and half == 1):
                    nc.scalar.copy(out=x_bf[gi][:, cols], in_=x_bytes_sb[:, gi, cols].bitcast(FP8))
                else:
                    nc.gpsimd.tensor_copy(out=x_bf[gi][:, cols], in_=x_bytes_sb[:, gi, cols].bitcast(FP8))

        def turn_and_scale(gi, half):
            both = slice(half * 2 * D, (half + 1) * 2 * D)
            turned = psum_turn.tile([P, D], F32, name="turned", tag="turn")
            for q2 in range(2):
                q = half * 2 + q2
                words = x_bf[gi][:, q * D : (q + 1) * D].bitcast(F32)
                for u in range(2):
                    c0 = (u * 2 + q2) * P
                    nc.tensor.transpose(out=turned[:, c0 : c0 + P], in_=words[:, u : D // 2 : 2], identity=token_perm[:])
            nc.vector.tensor_tensor(
                out=x_grouped[gi][:, both].rearrange("p (c u e) -> p c u e", u=2, e=2),
                in0=turned[:].bitcast(BF16).rearrange("p (u c e) -> p c u e", u=2, e=2),
                in1=scale_cols[:].rearrange("p (o u e) -> p o u e", o=1, u=2).to_broadcast([P, 2 * P, 2, 2]),
                op=ALU.mult,
            )

        def quantise_x(gi):
            nc.vector.quantize_mx(out=x_codes[gi][:].bitcast(FP8X4), scales=x_scales[gi][:], in_=x_grouped[gi][:])

        def second_table(gi):
            nc.vector.tensor_scalar(
                out=cos_msin[gi][:].bitcast(I32),
                in0=cos_sin[gi][:].bitcast(I32),
                scalar1=-0x80000000,
                scalar2=None,
                op0=ALU.bitwise_xor,
            )

        squares = {}
        gained = {}
        inv_rms = {}

        accs = {}

        def project(gi, h0):
            acc_pair = psum_acc.tile([P, 2, D], F32, name="acc_pair", tag="acc")
            for i in range(2):
                head = slice((h0 + i) * P, (h0 + i + 1) * P)
                nc.tensor.matmul_mx(
                    out=acc_pair[:, i, :],
                    lhsT=w_codes[:, head].bitcast(FP8X4),
                    lhsT_scale=w_scales[:, head],
                    rhs=x_codes[gi][:].bitcast(FP8X4),
                    rhs_scale=x_scales[gi][:],
                    start=True,
                    stop=True,
                )
                accs[gi, h0 + i] = acc_pair[:, i, :]

        def square(gi, h):
            square_h = per_head.tile([P, D], F32, name="square", tag="square")
            nc.scalar.activation(out=square_h[:], in_=accs[gi, h], func=ACT.Square, bias=b_and_g[:, h : h + 1], scale=1.0)
            squares[gi, h] = square_h

        def gain(gi, h):
            gained_h = per_head.tile([P, D], F32, name="gained", tag="gained")
            nc.scalar.activation(
                out=gained_h[:],
                in_=accs[gi, h],
                func=ACT.Identity,
                bias=b_times_g[:, h : h + 1],
                scale=b_and_g[:, HEADS + h : HEADS + h + 1],
            )
            gained[gi, h] = gained_h

        square_sums = {}

        def turn_squares(gi, half):
            if half == 0:
                square_sums_g = psum_sq.tile([P, D], F32, name="square_sums", tag="square_sums")
                square_sums[gi] = square_sums_g
            square_sums_g = square_sums[gi]
            for i in (2 * half, 2 * half + 1):
                for h in range(HEADS):
                    nc.tensor.matmul(
                        out=square_sums_g[:, i * P : (i + 1) * P],
                        lhsT=squares[gi, h][:, i * P : (i + 1) * P],
                        rhs=identity[:],
                        is_transpose=True,
                        start=(h == 0),
                        stop=(h == HEADS - 1),
                    )

        def rms(gi):
            total = per_group.tile([P, TILES], F32, name="total", tag="total")
            for i in range(TILES):
                unused = per_tile.tile([P, P], F32, name="unused", tag="unused")
                nc.scalar.activation(
                    out=unused[:], in_=square_sums[gi][:, i * P : (i + 1) * P], func=ACT.Copy, accum_out=total[:, i : i + 1]
                )
            inv_rms_g = per_group.tile([P, TILES], F32, name="inv_rms", tag="inv_rms")
            nc.scalar.activation(out=inv_rms_g[:], in_=total[:], func=ACT.Abs_reciprocal_sqrt, bias=EPS, scale=1.0 / D)
            inv_rms[gi] = inv_rms_g

        by_pair = [P, HEADS, PAIRS, 2]

        rope_tiles = {}

        def rope(tile):
            gi, q = tile // TILES, tile % TILES
            i = tile % 2
            if i == 0:
                products = []
                for e in range(2):
                    product = per_tile.tile([P, 2, D], F32, name="product%d" % e, tag="product%d" % e)
                    products.append(product)
                rope_tiles[tile // 2] = products
            products = rope_tiles[tile // 2]
            y_tokens = psum_turn.tile([P, D], F32, name="y_tokens", tag="turn")
            for h in range(HEADS):
                nc.tensor.transpose(
                    out=y_tokens[:, h * P : (h + 1) * P],
                    in_=gained[gi, h][:, q * P : (q + 1) * P],
                    identity=identity[:],
                )
            pairs = y_tokens[:].rearrange("p (h j e) -> p h j e", h=HEADS, e=2)
            for e, table, step in ((0, cos_sin[gi], 1), (1, cos_msin[gi], -1)):
                nc.vector.scalar_tensor_tensor(
                    out=products[e][:, i, :].rearrange("p (h j f) -> p h j f", h=HEADS, f=2)[:, :, :, ::step],
                    in0=pairs[:, :, :, e : e + 1].to_broadcast(by_pair),
                    scalar=inv_rms[gi][:, q : q + 1],
                    in1=table[:, q * P : (q + 1) * P].rearrange("p (o j f) -> p o j f", o=1, f=2).to_broadcast(by_pair),
                    op0=ALU.mult,
                    op1=ALU.mult,
                )
            if i == 0:
                rotated = per_tile.tile([P, 2, D], F32, name="rotated", tag="rotated")
                products.append(rotated)
            if tile < LAST_TILES:
                if i == 1:
                    rotated = products[2]
                    nc.gpsimd.tensor_tensor(out=rotated[:], in0=products[0][:], in1=products[1][:], op=ALU.add)
                    for i in range(2):
                        nc.sync.dma_start(out=out_by_tile[gi, q - 1 + i], in_=rotated[:, i, :])

        def add(tile, engine):
            p0, p1, rotated = rope_tiles[tile // 2]
            i = tile % 2
            engine.tensor_tensor(out=rotated[:, i, :], in0=p0[:, i, :], in1=p1[:, i, :], op=ALU.add)
            nc.sync.dma_start(out=out_by_tile[tile // TILES, tile % TILES], in_=rotated[:, i, :])

        cast(0, 0)
        cast(0, 1)
        copy_w()
        turn_and_scale(0, 0)
        turn_and_scale(0, 1)
        quantise_w()
        quantise_x(0)
        bias_and_gain_to_partitions()
        cast(1, 0)
        cast(1, 1)
        cast(2, 0)
        cast(2, 1)
        cast(3, 0)
        cast(3, 1)
        cast(4, 0)
        cast(4, 1)
        turn_and_scale(1, 0)
        turn_and_scale(1, 1)
        quantise_x(1)
        project(0, 0)
        project(0, 2)
        square(0, 0)
        square(0, 1)
        gain(0, 0)
        gain(0, 1)
        square(0, 2)
        square(0, 3)
        gain(0, 2)
        gain(0, 3)
        turn_and_scale(2, 0)
        turn_and_scale(2, 1)
        quantise_x(2)
        turn_and_scale(3, 0)
        second_table(0)
        second_table(1)
        second_table(2)
        second_table(3)
        second_table(4)
        project(1, 0)
        square(1, 0)
        square(1, 1)
        turn_squares(0, 0)
        turn_squares(0, 1)
        rms(0)
        gain(1, 0)
        gain(1, 1)
        turn_and_scale(3, 1)
        rope(0)
        project(1, 2)
        square(1, 2)
        square(1, 3)
        gain(1, 2)
        gain(1, 3)
        rope(1)
        quantise_x(3)
        project(2, 0)
        square(2, 0)
        square(2, 1)
        rope(2)
        turn_squares(1, 0)
        turn_squares(1, 1)
        rms(1)
        gain(2, 0)
        gain(2, 1)
        rope(3)
        project(2, 2)
        square(2, 2)
        square(2, 3)
        gain(2, 2)
        gain(2, 3)
        rope(4)
        turn_and_scale(4, 0)
        turn_and_scale(4, 1)
        project(3, 0)
        square(3, 0)
        square(3, 1)
        rope(5)
        quantise_x(4)
        turn_squares(2, 0)
        turn_squares(2, 1)
        rms(2)
        gain(3, 0)
        gain(3, 1)
        rope(6)
        project(3, 2)
        square(3, 2)
        square(3, 3)
        gain(3, 2)
        gain(3, 3)
        rope(7)
        rope(8)
        rope(9)
        project(4, 0)
        square(4, 0)
        square(4, 1)
        rope(10)
        turn_squares(3, 0)
        turn_squares(3, 1)
        rms(3)
        rope(11)
        rope(12)
        project(4, 2)
        square(4, 2)
        square(4, 3)
        gain(4, 0)
        gain(4, 1)
        gain(4, 2)
        gain(4, 3)
        rope(13)
        rope(14)
        turn_squares(4, 0)
        turn_squares(4, 1)
        rope(15)
        rms(4)
        rope(16)
        rope(17)
        add(16, nc.gpsimd)
        rope(18)
        rope(19)
        add(17, nc.vector)
        add(18, nc.vector)
        add(19, nc.vector)
